import numpy as np
import ml_dtypes


def mxq(x, axis, fmt="e4m3"):
    dtype, down = {"e4m3": (ml_dtypes.float8_e4m3fn, 7), "e5m2": (ml_dtypes.float8_e5m2, 14)}[fmt]
    v = np.moveaxis(np.asarray(x, np.float32).astype(ml_dtypes.bfloat16).astype(np.float64), axis, -1)
    blocks = v.reshape(v.shape[:-1] + (-1, 32))
    amax = np.abs(blocks).max(-1, keepdims=True)
    byte = np.maximum(np.where(amax > 0, np.frexp(amax)[1] - 1 + 127, 0) - down, 1)
    scale = np.exp2(byte - 127.0)
    codes = (blocks / scale).astype(np.float32).astype(dtype).astype(np.float64)
    return np.moveaxis((codes * scale).reshape(v.shape), -1, axis)


WIDE = False


def mx_kscale(k):
    if not WIDE:
        return np.ones(k)
    levels = np.array([10, -10, 5, -5, 0])
    if k % 512:
        return np.exp2(np.random.permutation(np.resize(levels, k // 32))).repeat(32)
    a = np.empty((k // 512, 16))
    for p in range(k // 512):
        a[p, :8] = np.random.permutation(np.resize(levels, 8))
        for g in range(8):
            far = levels[np.abs(levels - a[p, g]) >= 10]
            a[p, g + 8] = far[np.random.randint(len(far))]
    return np.exp2(a.ravel()).repeat(32)


BF16 = ml_dtypes.bfloat16


def bf(x):
    return np.asarray(x, np.float32).astype(BF16)


def f64(x):
    return np.asarray(x).astype(np.float64)


M, B, I, H, O = 5, 2048, 128, 512, 64
O2 = 2 * O
EPS = 1e-6


def softplus(v):
    return np.maximum(v, 0.0) + np.log(1.0 + np.exp(-np.abs(v)))


def setup_inputs():
    s, t = mx_kscale(H), mx_kscale(H)
    return {"h1": bf(np.maximum(np.random.standard_normal((M, B, H)), 0.0) * s),
            "W2": bf(np.random.standard_normal((M, H, H)) * 1.4 / np.sqrt(H) * t[None, :, None] / s[None, None, :]),
            "b2": bf(np.random.standard_normal((M, H)) * 0.3 * t),
            "W3": bf(np.random.standard_normal((M, O2, H)) * 1.4 / np.sqrt(H) / t[None, None, :]),
            "b3": bf(np.random.standard_normal((M, O2)) * 0.3)}


def reference(h1, W2, b2, W3, b3):
    h2 = np.maximum(f64(bf(mxq(f64(h1), 2, "e4m3") @ mxq(f64(W2), 2, "e4m3").transpose(0, 2, 1))) + f64(b2)[:, None, :], 0.0)
    y = (mxq(h2, 2, "e4m3") @ mxq(f64(W3), 2, "e4m3").transpose(0, 2, 1)) + f64(b3)[:, None, :]
    means = y[:, :, :O]
    variances = softplus(y[:, :, O:]) + EPS
    mean = means.mean(axis=0)
    variance = (variances + means ** 2).mean(axis=0) - mean ** 2
    variance = np.maximum(variance, 0.0) + EPS
    return mean, variance

@@ -1,0 +1,443 @@
+from contextlib import ExitStack
+
+import concourse.mybir as mybir
+from concourse.masks import make_identity
+
+NM, B, H, O = 5, 2048, 512, 64
+O2 = 2 * O
+FLOPS = 2 * NM * B * H * (H + O2)
+
+F32 = mybir.dt.float32
+BF16 = mybir.dt.bfloat16
+U32 = mybir.dt.uint32
+U8 = mybir.dt.uint8
+FP8X4 = mybir.dt.float8_e4m3fn_x4
+ACT = mybir.ActivationFunctionType
+ALU = mybir.AluOpType
+
+P = 128
+CH = 512
+NCH = B // CH
+NS = NCH * NM
+RAW_BUFS = 8
+BANK_DT = BF16
+
+
+def tile_gaussianmixturemlp_pa_kernel(tc, h1, W2, b2, W3, b3, out_0, out_1):
+    nc = tc.nc
+    with ExitStack() as ctx:
+        const = ctx.enter_context(tc.tile_pool(name="const", bufs=1))
+        rawp = ctx.enter_context(tc.tile_pool(name="rawp", bufs=RAW_BUFS))
+        work = ctx.enter_context(tc.tile_pool(name="work", bufs=2))
+        tp = ctx.enter_context(tc.psum_pool(name="tp", bufs=2))
+        s1 = ctx.enter_context(tc.psum_pool(name="s1", bufs=4))
+        s2 = ctx.enter_context(tc.psum_pool(name="s2", bufs=1))
+        aux = ctx.enter_context(tc.psum_pool(name="aux", bufs=1))
+        ctx.enter_context(tc.manual_schedule())
+
+        ident = const.tile([P, P], F32, name="ident", tag="ident")
+        warm = const.tile([P, 1], F32, name="warm", tag="warm")
+        warm2 = const.tile([P, 1], F32, name="warm2", tag="warm2")
+        b2c = const.tile([P, NM, 4], BF16, name="b2c", tag="b2c")
+        b3b = const.tile([P, NM, O2], BF16, name="b3b", tag="b3b")
+        w3raw = const.tile([P, NM, H], BF16, name="w3raw", tag="w3raw")
+        w3g = const.tile([P, NM * O2, 4], BF16, name="w3g", tag="w3g", align_bytes=64)
+        w2c = const.tile([P, NM, H], U32, name="w2c", tag="w2c", align_bytes=64)
+        w2s = const.tile([P, NM, H], U8, name="w2s", tag="w2s", align_bytes=64)
+        w3c = const.tile([P, NM * O2], U32, name="w3c", tag="w3c", align_bytes=64)
+        w3s = const.tile([P, NM * O2], U8, name="w3s", tag="w3s", align_bytes=64)
+        accp = const.tile([P, NCH, 4, O], F32, name="accp", tag="accp")
+        upre = const.tile([P, NCH, 4, O], F32, name="upre", tag="upre")
+        lnp = const.tile([P, NCH, 4, O], F32, name="lnp", tag="lnp")
+        wv = const.tile([P, NCH, 4, O], F32, name="wv", tag="wv")
+        var_sb = const.tile([P, NCH, 4, O], F32, name="var_sb", tag="var_sb")
+        bsum = const.tile([P, O], F32, name="bsum", tag="bsum")
+        bbar = const.tile([P, 1, O], F32, name="bbar", tag="bbar")
+
+        zl = const.tile([P, P], BF16, name="zl", tag="zl")
+        zr = const.tile([P, CH], BF16, name="zr", tag="zr")
+        nc.vector.memset(zl[:], 0.0)
+        nc.vector.memset(zr[:], 0.0)
+        nc.vector.memset(warm[:], 0.0)
+        nc.scalar.activation(out=warm2[:], in_=warm[:], func=ACT.Exp)
+        make_identity(nc, ident[:])
+        nc.scalar.dma_start(out=b2c[:], in_=b2.rearrange("m (p t) -> p m t", t=4))
+
+        raw_w2 = {}
+        raw_h1 = {}
+        loads = [("w2", 0), ("h1", 0), ("h1", 1), ("w2", 1), ("h1", 2), ("w3", 0)]
+        for i in range(2, NM):
+            loads.append(("w2", i))
+            loads.append(("h1", i + 1))
+        for i in range(NM + 1, NS):
+            loads.append(("h1", i))
+        state = {"next": 0, "slots": RAW_BUFS}
+
+        def pump():
+            while state["next"] < len(loads):
+                kind, i = loads[state["next"]]
+                if kind == "w3":
+                    nc.sync.dma_start(out=w3raw[:], in_=W3.rearrange("m o k -> o m k"))
+                else:
+                    if state["slots"] == 0:
+                        return
+                    state["slots"] = state["slots"] - 1
+                    t = rawp.tile([P, 4, H], BF16, name="raw_%s%d" % (kind, i), tag="raw")
+                    if kind == "w2":
+                        nc.sync.dma_start(out=t[:], in_=W2[i].rearrange("(p t) k -> p t k", t=4))
+                        raw_w2[i] = t
+                    else:
+                        c, m = i // NM, i % NM
+                        nc.sync.dma_start(
+                            out=t[:],
+                            in_=h1[m, c * CH:(c + 1) * CH, :].rearrange("(p j) k -> p j k", j=4),
+                        )
+                        raw_h1[i] = t
+                state["next"] = state["next"] + 1
+
+        def freed():
+            state["slots"] = state["slots"] + 1
+            pump()
+
+        def transposes(pool, tag, words, w_first, count):
+            xt = pool.tile([P, 2, 256], F32, name="xt_%s" % tag, tag=tag)
+            for jj in range(count):
+                w0 = w_first + 256 * jj
+                for u in range(2):
+                    nc.tensor.transpose(
+                        xt[:, u, P * jj:P * (jj + 1)], words[:, w0 + u:w0 + 256:2], ident[:]
+                    )
+            return xt
+
+        def copy_out(on_scalar, grouped, n0, xt, ncols):
+            gw = grouped[:].rearrange("p n t -> p (n t)").bitcast(F32)
+            dst = gw[:, 2 * n0:2 * (n0 + ncols)].rearrange("p (r u) -> p r u", u=2)
+            src = xt[:, :, 0:ncols].rearrange("p u r -> p r u")
+            if on_scalar:
+                nc.scalar.copy(out=dst, in_=src)
+            else:
+                nc.vector.tensor_copy(out=dst, in_=src)
+
+        def words_of(t):
+            return t[:].rearrange("p j k -> p (j k)").bitcast(F32)
+
+        xt_h1 = {}
+        g1 = {}
+        c1 = {}
+        sc1 = {}
+        bank = {}
+        h2raw = {}
+        g2 = {}
+        c2 = {}
+        sc2 = {}
+        pbank = {}
+        ys = {}
+        sqs = {}
+        exs = {}
+        accs = {}
+        psums = {}
+        means = {}
+        msqs = {}
+        wgs = {}
+        xt_w = {}
+
+        def st_a(s, half):
+            if half == 0:
+                xt_h1[s] = []
+            xt_h1[s].append(transposes(tp, "xt", words_of(raw_h1[s]), 512 * half, 2))
+            if half == 1:
+                freed()
+
+        def st_b(s):
+            g1[s] = work.tile([P, CH, 4], BF16, name="g1", tag="g1", bufs=2, align_bytes=64)
+            for half in range(2):
+                copy_out(True, g1[s], 256 * half, xt_h1[s][half], 256)
+
+        def st_c(s):
+            c1[s] = work.tile([P, CH], U32, name="c1", tag="c1", bufs=3, align_bytes=64)
+            sc1[s] = work.tile([P, CH], U8, name="sc1", tag="sc1", bufs=3, align_bytes=64)
+            nc.vector.quantize_mx(
+                out=c1[s][:].bitcast(FP8X4), scales=sc1[s][:],
+                in_=g1[s][:].rearrange("p n t -> p (n t)"),
+            )
+
+        def st_d(s, ts):
+            m = s % NM
+            if ts[0] == 0:
+                bank[s] = []
+            for t in ts:
+                ps = s1.tile([P, CH], BANK_DT, name="bank", tag="bank")
+                nc.tensor.matmul_mx(
+                    out=ps[:],
+                    lhsT=w2c[:, m, P * t:P * (t + 1)].bitcast(FP8X4),
+                    lhsT_scale=w2s[:, m, P * t:P * (t + 1)],
+                    rhs=c1[s][:].bitcast(FP8X4),
+                    rhs_scale=sc1[s][:],
+                    start=True, stop=True,
+                )
+                bank[s].append(ps)
+
+        def st_e(s):
+            m = s % NM
+            h2raw[s] = work.tile([P, 4, CH], BF16, name="h2raw", tag="h2raw", bufs=3)
+            for t in range(4):
+                nc.scalar.activation(
+                    out=h2raw[s][:, t, :], in_=bank[s][t][:], func=ACT.Relu,
+                    bias=b2c[:, m, t:t + 1], scale=1.0,
+                )
+
+        def st_f(s):
+            g2[s] = work.tile([P, CH, 4], BF16, name="g2", tag="g2", bufs=2, align_bytes=64)
+            nc.vector.tensor_copy(out=g2[s][:], in_=h2raw[s][:].rearrange("p t n -> p n t"))
+
+        def st_g(s):
+            c2[s] = work.tile([P, CH], U32, name="c2", tag="c2", bufs=7, align_bytes=64)
+            sc2[s] = work.tile([P, CH], U8, name="sc2", tag="sc2", bufs=7, align_bytes=64)
+            nc.vector.quantize_mx(
+                out=c2[s][:].bitcast(FP8X4), scales=sc2[s][:],
+                in_=g2[s][:].rearrange("p n t -> p (n t)"),
+            )
+
+        def plain_dummy(n):
+            for i in range(n):
+                junk = s1.tile([P, CH], F32, name="junk", tag="bank")
+                nc.tensor.matmul(out=junk[:], lhsT=zl[:], rhs=zr[:], start=True, stop=True)
+
+        def get_pbank(s):
+            if s not in pbank:
+                pbank[s] = s2.tile([P, 4, O2], F32, name="pbank", tag="pbank")
+            return pbank[s]
+
+        def mx_dummy(s):
+            nc.tensor.matmul_mx(
+                out=get_pbank(s)[:].rearrange("p j o -> p (j o)"),
+                lhsT=c2[s - 1][:, 0:P].bitcast(FP8X4),
+                lhsT_scale=sc2[s - 1][:, 0:P],
+                rhs=w3c[:, 0:CH].bitcast(FP8X4),
+                rhs_scale=w3s[:, 0:CH],
+                start=True, stop=True,
+            )
+
+        def st_h(s):
+            m = s % NM
+            get_pbank(s)
+            for j in range(4):
+                nc.tensor.matmul_mx(
+                    out=pbank[s][:, j, :],
+                    lhsT=c2[s][:, P * j:P * (j + 1)].bitcast(FP8X4),
+                    lhsT_scale=sc2[s][:, P * j:P * (j + 1)],
+                    rhs=w3c[:, O2 * m:O2 * (m + 1)].bitcast(FP8X4),
+                    rhs_scale=w3s[:, O2 * m:O2 * (m + 1)],
+                    start=True, stop=True,
+                )
+
+        def st_hsum(c):
+            psums[c] = aux.tile([P, 4, O2], F32, name="psum_all", tag="xw")
+            for j in range(4):
+                for m in range(NM):
+                    s = c * NM + m
+                    nc.tensor.matmul_mx(
+                        out=psums[c][:, j, :],
+                        lhsT=c2[s][:, P * j:P * (j + 1)].bitcast(FP8X4),
+                        lhsT_scale=sc2[s][:, P * j:P * (j + 1)],
+                        rhs=w3c[:, O2 * m:O2 * (m + 1)].bitcast(FP8X4),
+                        rhs_scale=w3s[:, O2 * m:O2 * (m + 1)],
+                        start=(m == 0), stop=(m == NM - 1),
+                    )
+
+        def bias_mean():
+            nc.vector.tensor_reduce(
+                out=bsum[:], in_=b3b[:, :, 0:O].rearrange("p m o -> p o m"),
+                axis=mybir.AxisListType.X, op=ALU.add)
+            nc.vector.tensor_scalar(
+                out=bbar[:, 0, :], in0=bsum[:], scalar1=0.2, scalar2=None, op0=ALU.mult)
+
+        def st_i(s):
+            m = s % NM
+            ys[s] = work.tile([P, 4, O2], F32, name="ys", tag="ys", bufs=4)
+            nc.vector.tensor_tensor(
+                out=ys[s][:], in0=pbank[s][:],
+                in1=b3b[:, m:m + 1, :].to_broadcast([P, 4, O2]), op=ALU.add,
+            )
+
+        def st_js(s):
+            sqs[s] = work.tile([P, 4, O], F32, name="sqs", tag="sqs", bufs=2)
+            ab = work.tile([P, 4, O], F32, name="ab", tag="ab", bufs=2)
+            exs[s] = work.tile([P, 4, O], F32, name="exs", tag="exs", bufs=2)
+            nc.scalar.activation(out=ab[:], in_=ys[s][:, :, O:O2], func=ACT.Abs)
+            nc.scalar.activation(out=sqs[s][:], in_=ys[s][:, :, 0:O], func=ACT.Square)
+            nc.scalar.activation(out=exs[s][:], in_=ab[:], func=ACT.Exp, scale=-1.0)
+
+        def st_mean(c):
+            means[c] = work.tile([P, 4, O], F32, name="mean_sb", tag="mean_sb", bufs=2)
+            msqs[c] = work.tile([P, 4, O], F32, name="msq", tag="msq", bufs=2)
+            nc.vector.scalar_tensor_tensor(
+                out=means[c][:], in0=psums[c][:, :, 0:O], scalar=0.2,
+                in1=bbar[:].to_broadcast([P, 4, O]), op0=ALU.mult, op1=ALU.add)
+            nc.sync.dma_start(
+                out=out_0[c * CH:(c + 1) * CH, :].rearrange("(p j) o -> p j o", j=4),
+                in_=means[c][:])
+
+        def st_msq(c):
+            nc.vector.tensor_tensor(out=msqs[c][:], in0=means[c][:], in1=means[c][:], op=ALU.mult)
+
+        def st_u(c):
+            nc.vector.scalar_tensor_tensor(
+                out=upre[:, c], in0=accs[c][:], scalar=0.2, in1=msqs[c][:],
+                op0=ALU.mult, op1=ALU.subtract)
+
+        def st_jv(s):
+            c, m = s // NM, s % NM
+            v = ys[s][:, :, O:O2]
+            if m == 0:
+                accs[c] = work.tile([P, 4, O], F32, name="accs", tag="accs", bufs=2)
+                nc.vector.tensor_scalar(
+                    out=accp[:, c], in0=exs[s][:], scalar1=1.0, scalar2=None, op0=ALU.add)
+                nc.vector.scalar_tensor_tensor(
+                    out=accs[c][:], in0=v, scalar=0.0, in1=sqs[s][:], op0=ALU.max, op1=ALU.add)
+                return
+            nc.vector.scalar_tensor_tensor(
+                out=accs[c][:], in0=v, scalar=0.0, in1=accs[c][:], op0=ALU.max, op1=ALU.add)
+            nc.vector.scalar_tensor_tensor(
+                out=accp[:, c], in0=exs[s][:], scalar=1.0, in1=accp[:, c], op0=ALU.add, op1=ALU.mult)
+            nc.vector.tensor_tensor(out=accs[c][:], in0=sqs[s][:], in1=accs[c][:], op=ALU.add)
+
+        def flat(t, c0, c1_):
+            return t[:, c0:c1_].rearrange("p c j o -> p (c j o)")
+
+        def fin_ln(c0, c1_):
+            nc.scalar.activation(out=flat(lnp, c0, c1_), in_=flat(accp, c0, c1_), func=ACT.Ln)
+
+        def fin_w(c0, c1_):
+            nc.vector.scalar_tensor_tensor(
+                out=flat(wv, c0, c1_), in0=flat(lnp, c0, c1_), scalar=0.2, in1=flat(upre, c0, c1_),
+                op0=ALU.mult, op1=ALU.add)
+
+        def fin_v(c0, c1_):
+            nc.vector.tensor_scalar(
+                out=flat(var_sb, c0, c1_), in0=flat(wv, c0, c1_), scalar1=-1e-6, scalar2=2e-6,
+                op0=ALU.max, op1=ALU.add)
+            nc.sync.dma_start(
+                out=out_1.rearrange("(c p j) o -> p c (j o)", c=NCH, j=4)[:, c0:c1_, :],
+                in_=var_sb[:, c0:c1_].rearrange("p c j o -> p c (j o)"))
+
+        def w2_t(m, half):
+            xt_w[(m, half)] = transposes(aux, "xw", words_of(raw_w2[m]), 512 * half, 2)
+            if half == 1:
+                freed()
+
+        def w2_copy(m, half):
+            if half == 0:
+                wgs[m] = work.tile([P, H, 4], BF16, name="wg", tag="wg", bufs=2, align_bytes=64)
+            copy_out(half == 0, wgs[m], 256 * half, xt_w[(m, half)], 256)
+
+        def w2_q(m):
+            nc.vector.quantize_mx(
+                out=w2c[:, m, :].bitcast(FP8X4), scales=w2s[:, m, :],
+                in_=wgs[m][:].rearrange("p n t -> p (n t)"),
+            )
+
+        def w3_prep(q):
+            count = min(2, NM - 2 * q)
+            ncols = P * count
+            w = w3raw[:].rearrange("p m k -> p (m k)").bitcast(F32)
+            xt = transposes(aux, "xw", w, 512 * q, count)
+            copy_out(False, w3g, 256 * q, xt, ncols)
+            nc.vector.quantize_mx(
+                out=w3c[:, 256 * q:256 * q + ncols].bitcast(FP8X4),
+                scales=w3s[:, 256 * q:256 * q + ncols],
+                in_=w3g[:].rearrange("p n t -> p (n t)")[:, 1024 * q:1024 * q + 4 * ncols],
+            )
+
+        def ok(s):
+            return 0 <= s < NS
+
+        pump()
+        plain_dummy(6)
+        w2_t(0, 0)
+        w2_copy(0, 0)
+        plain_dummy(2)
+        w2_t(0, 1)
+        w2_copy(0, 1)
+        w2_q(0)
+        plain_dummy(2)
+        st_a(0, 0)
+        st_a(0, 1)
+        plain_dummy(2)
+        for k in range(-1, NS + 3):
+            wm = k + 1
+            has_w = 1 <= wm < NM
+            junk_ok = 2 <= k <= NS
+            chunk_mean = ok(k - 2) and (k - 2) % NM == NM - 1
+            if ok(k + 1):
+                st_b(k + 1)
+            if k == 0:
+                nc.scalar.dma_start(
+                    out=b3b[:].rearrange("p m o -> p (m o)"),
+                    in_=b3.rearrange("m o -> (m o)").partition_broadcast(P),
+                )
+            if ok(k - 2) and k < NS:
+                st_i(k - 2)
+            if ok(k - 4) and (k - 4) % NM == NM - 1:
+                st_u((k - 4) // NM)
+            if k == 3:
+                bias_mean()
+            if chunk_mean and k < NS:
+                st_mean((k - 2) // NM)
+            if ok(k - 1):
+                st_f(k - 1)
+            if ok(k - 2) and k >= NS:
+                st_i(k - 2)
+            if chunk_mean and k >= NS:
+                st_mean((k - 2) // NM)
+            if ok(k + 1):
+                st_c(k + 1)
+            if chunk_mean and k < NS:
+                st_msq((k - 2) // NM)
+            if ok(k):
+                st_d(k, [0, 1])
+            if has_w:
+                w2_t(wm, 0)
+                w2_copy(wm, 0)
+            if ok(k + 2):
+                st_a(k + 2, 0)
+            if ok(k):
+                st_d(k, [2])
+            if junk_ok:
+                mx_dummy(k - 1)
+            if has_w:
+                w2_t(wm, 1)
+                w2_copy(wm, 1)
+            if ok(k - 1):
+                st_g(k - 1)
+            if has_w:
+                w2_q(wm)
+            if ok(k + 2):
+                st_a(k + 2, 1)
+            if ok(k):
+                st_d(k, [3])
+            if 0 <= k < 3:
+                w3_prep(k)
+            if junk_ok:
+                mx_dummy(k - 1)
+            if ok(k - 1):
+                st_h(k - 1)
+                if (k - 1) % NM == NM - 1:
+                    st_hsum((k - 1) // NM)
+            if k < 0:
+                plain_dummy(2)
+            if ok(k - 3):
+                st_js(k - 3)
+            if ok(k):
+                st_e(k)
+            if ok(k - 3):
+                st_jv(k - 3)
+            if chunk_mean and k >= NS:
+                st_msq((k - 2) // NM)
+        st_u(NCH - 1)
+        fin_ln(0, NCH - 1)
+        fin_ln(NCH - 1, NCH)
+        fin_w(0, NCH - 1)
+        fin_w(NCH - 1, NCH)
+        fin_v(0, NCH - 1)
+        fin_v(NCH - 1, NCH)

@@ -208,16 +208,6 @@ def tile_gaussianmixturemlp_pa_kernel(tc, h1, W2, b2, W3, b3, out_0, out_1):
                 pbank[s] = s2.tile([P, 4, O2], F32, name="pbank", tag="pbank")
             return pbank[s]
 
-        def mx_dummy(s):
-            nc.tensor.matmul_mx(
-                out=get_pbank(s)[:].rearrange("p j o -> p (j o)"),
-                lhsT=c2[s - 1][:, 0:P].bitcast(FP8X4),
-                lhsT_scale=sc2[s - 1][:, 0:P],
-                rhs=w3c[:, 0:CH].bitcast(FP8X4),
-                rhs_scale=w3s[:, 0:CH],
-                start=True, stop=True,
-            )
-
         def st_h(s):
             m = s % NM
             get_pbank(s)
@@ -367,7 +357,6 @@ def tile_gaussianmixturemlp_pa_kernel(tc, h1, W2, b2, W3, b3, out_0, out_1):
         for k in range(-1, NS + 3):
             wm = k + 1
             has_w = 1 <= wm < NM
-            junk_ok = 2 <= k <= NS
             chunk_mean = ok(k - 2) and (k - 2) % NM == NM - 1
             if ok(k + 1):
                 st_b(k + 1)
@@ -403,8 +392,6 @@ def tile_gaussianmixturemlp_pa_kernel(tc, h1, W2, b2, W3, b3, out_0, out_1):
                 st_a(k + 2, 0)
             if ok(k):
                 st_d(k, [2])
-            if junk_ok:
-                mx_dummy(k - 1)
             if has_w:
                 w2_t(wm, 1)
                 w2_copy(wm, 1)
@@ -418,8 +405,6 @@ def tile_gaussianmixturemlp_pa_kernel(tc, h1, W2, b2, W3, b3, out_0, out_1):
                 st_d(k, [3])
             if 0 <= k < 3:
                 w3_prep(k)
-            if junk_ok:
-                mx_dummy(k - 1)
             if ok(k - 1):
                 st_h(k - 1)
                 if (k - 1) % NM == NM - 1:

@@ -11,6 +11,7 @@ F32 = mybir.dt.float32
 BF16 = mybir.dt.bfloat16
 U32 = mybir.dt.uint32
 U8 = mybir.dt.uint8
+I32 = mybir.dt.int32
 FP8X4 = mybir.dt.float8_e4m3fn_x4
 ACT = mybir.ActivationFunctionType
 ALU = mybir.AluOpType
@@ -19,6 +20,9 @@ P = 128
 CH = 512
 NCH = B // CH
 NS = NCH * NM
+HALF = CH // 2
+VFROM = 4
+W3COLS = O * (4 * NM + 1)
 RAW_BUFS = 8
 BANK_DT = BF16
 
@@ -39,29 +43,44 @@ def tile_gaussianmixturemlp_pa_kernel(tc, h1, W2, b2, W3, b3, out_0, out_1):
         warm = const.tile([P, 1], F32, name="warm", tag="warm")
         warm2 = const.tile([P, 1], F32, name="warm2", tag="warm2")
         b2c = const.tile([P, NM, 4], BF16, name="b2c", tag="b2c")
-        b3b = const.tile([P, NM, O2], BF16, name="b3b", tag="b3b")
+        identb = const.tile([P, P], BF16, name="identb", tag="identb")
+        b3in = const.tile([P, P], BF16, name="b3in", tag="b3in")
+        b3t = const.tile([P, 2 * NM], F32, name="b3t", tag="b3t")
+        nbr = const.tile([P, NM], F32, name="nbr", tag="nbr")
+        bs = const.tile([P, 2], F32, name="bs", tag="bs")
+        bbar = const.tile([P, 1], F32, name="bbar", tag="bbar")
+        vlo = const.tile([P, 1], F32, name="vlo", tag="vlo")
+        vadd = const.tile([P, 1], F32, name="vadd", tag="vadd")
         w3raw = const.tile([P, NM, H], BF16, name="w3raw", tag="w3raw")
         w3g = const.tile([P, NM * O2, 4], BF16, name="w3g", tag="w3g", align_bytes=64)
         w2c = const.tile([P, NM, H], U32, name="w2c", tag="w2c", align_bytes=64)
         w2s = const.tile([P, NM, H], U8, name="w2s", tag="w2s", align_bytes=64)
-        w3c = const.tile([P, NM * O2], U32, name="w3c", tag="w3c", align_bytes=64)
-        w3s = const.tile([P, NM * O2], U8, name="w3s", tag="w3s", align_bytes=64)
-        accp = const.tile([P, NCH, 4, O], F32, name="accp", tag="accp")
-        upre = const.tile([P, NCH, 4, O], F32, name="upre", tag="upre")
-        lnp = const.tile([P, NCH, 4, O], F32, name="lnp", tag="lnp")
-        wv = const.tile([P, NCH, 4, O], F32, name="wv", tag="wv")
+        w3c = const.tile([P, W3COLS], U32, name="w3c", tag="w3c", align_bytes=64)
+        w3s = const.tile([P, W3COLS], U8, name="w3s", tag="w3s", align_bytes=64)
+        accp = const.tile([P, NCH, HALF], F32, name="accp", tag="accp")
+        upre = const.tile([P, NCH, HALF], F32, name="upre", tag="upre")
+        lnp = const.tile([P, NCH, HALF], F32, name="lnp", tag="lnp")
+        wv = const.tile([P, NCH, HALF], F32, name="wv", tag="wv")
+        var_t = const.tile([P, NCH, HALF], F32, name="var_t", tag="var_t")
         var_sb = const.tile([P, NCH, 4, O], F32, name="var_sb", tag="var_sb")
-        bsum = const.tile([P, O], F32, name="bsum", tag="bsum")
-        bbar = const.tile([P, 1, O], F32, name="bbar", tag="bbar")
 
         zl = const.tile([P, P], BF16, name="zl", tag="zl")
         zr = const.tile([P, CH], BF16, name="zr", tag="zr")
         nc.vector.memset(zl[:], 0.0)
         nc.vector.memset(zr[:], 0.0)
         nc.vector.memset(warm[:], 0.0)
+        nc.vector.memset(b3in[:], 0.0)
+        nc.vector.memset(w3c[:].bitcast(I32), 0)
+        nc.vector.memset(w3s[:].bitcast(I32), 0)
         nc.scalar.activation(out=warm2[:], in_=warm[:], func=ACT.Exp)
         make_identity(nc, ident[:])
+        make_identity(nc, identb[:])
         nc.scalar.dma_start(out=b2c[:], in_=b2.rearrange("m (p t) -> p m t", t=4))
+        for kind in range(2):
+            for h in range(2):
+                nc.scalar.dma_start(
+                    out=b3in[NM * kind:NM * (kind + 1), O * h:O * (h + 1)],
+                    in_=b3[:, O * kind:O * (kind + 1)])
 
         raw_w2 = {}
         raw_h1 = {}
@@ -130,13 +149,14 @@ def tile_gaussianmixturemlp_pa_kernel(tc, h1, W2, b2, W3, b3, out_0, out_1):
         g2 = {}
         c2 = {}
         sc2 = {}
-        pbank = {}
-        ys = {}
+        xy = {}
+        abs_ = {}
         sqs = {}
         exs = {}
         accs = {}
         psums = {}
         means = {}
+        mts = {}
         msqs = {}
         wgs = {}
         xt_w = {}
@@ -177,14 +197,21 @@ def tile_gaussianmixturemlp_pa_kernel(tc, h1, W2, b2, W3, b3, out_0, out_1):
                 )
                 bank[s].append(ps)
 
-        def st_e(s):
+        def st_e(s, ts):
             m = s % NM
-            h2raw[s] = work.tile([P, 4, CH], BF16, name="h2raw", tag="h2raw", bufs=3)
-            for t in range(4):
-                nc.scalar.activation(
-                    out=h2raw[s][:, t, :], in_=bank[s][t][:], func=ACT.Relu,
-                    bias=b2c[:, m, t:t + 1], scale=1.0,
-                )
+            if ts[0] == 0:
+                h2raw[s] = work.tile([P, 4, CH], BF16, name="h2raw", tag="h2raw", bufs=3)
+            for t in ts:
+                if t == 3 and s >= VFROM:
+                    nc.vector.tensor_scalar(
+                        out=h2raw[s][:, t, :], in0=bank[s][t][:], scalar1=b2c[:, m, t:t + 1], scalar2=0.0,
+                        op0=ALU.add, op1=ALU.max,
+                    )
+                else:
+                    nc.scalar.activation(
+                        out=h2raw[s][:, t, :], in_=bank[s][t][:], func=ACT.Relu,
+                        bias=b2c[:, m, t:t + 1], scale=1.0,
+                    )
 
         def st_f(s):
             g2[s] = work.tile([P, CH, 4], BF16, name="g2", tag="g2", bufs=2, align_bytes=64)
@@ -203,70 +230,122 @@ def tile_gaussianmixturemlp_pa_kernel(tc, h1, W2, b2, W3, b3, out_0, out_1):
                 junk = s1.tile([P, CH], F32, name="junk", tag="bank")
                 nc.tensor.matmul(out=junk[:], lhsT=zl[:], rhs=zr[:], start=True, stop=True)
 
-        def get_pbank(s):
-            if s not in pbank:
-                pbank[s] = s2.tile([P, 4, O2], F32, name="pbank", tag="pbank")
-            return pbank[s]
+        def w3_window(m, kind, h):
+            c0 = O * (4 * m + 2 * kind + 1 - h)
+            return slice(c0, c0 + P)
 
-        def st_h(s):
-            m = s % NM
-            get_pbank(s)
-            for j in range(4):
-                nc.tensor.matmul_mx(
-                    out=pbank[s][:, j, :],
-                    lhsT=c2[s][:, P * j:P * (j + 1)].bitcast(FP8X4),
-                    lhsT_scale=sc2[s][:, P * j:P * (j + 1)],
-                    rhs=w3c[:, O2 * m:O2 * (m + 1)].bitcast(FP8X4),
-                    rhs_scale=w3s[:, O2 * m:O2 * (m + 1)],
-                    start=True, stop=True,
-                )
-
-        def st_hsum(c):
-            psums[c] = aux.tile([P, 4, O2], F32, name="psum_all", tag="xw")
-            for j in range(4):
-                for m in range(NM):
-                    s = c * NM + m
-                    nc.tensor.matmul_mx(
-                        out=psums[c][:, j, :],
-                        lhsT=c2[s][:, P * j:P * (j + 1)].bitcast(FP8X4),
-                        lhsT_scale=sc2[s][:, P * j:P * (j + 1)],
-                        rhs=w3c[:, O2 * m:O2 * (m + 1)].bitcast(FP8X4),
-                        rhs_scale=w3s[:, O2 * m:O2 * (m + 1)],
-                        start=(m == 0), stop=(m == NM - 1),
-                    )
-
-        def bias_mean():
-            nc.vector.tensor_reduce(
-                out=bsum[:], in_=b3b[:, :, 0:O].rearrange("p m o -> p o m"),
-                axis=mybir.AxisListType.X, op=ALU.add)
-            nc.vector.tensor_scalar(
-                out=bbar[:, 0, :], in0=bsum[:], scalar1=0.2, scalar2=None, op0=ALU.mult)
-
-        def st_i(s):
-            m = s % NM
-            ys[s] = work.tile([P, 4, O2], F32, name="ys", tag="ys", bufs=4)
-            nc.vector.tensor_tensor(
-                out=ys[s][:], in0=pbank[s][:],
-                in1=b3b[:, m:m + 1, :].to_broadcast([P, 4, O2]), op=ALU.add,
+        def stage2_pass(out, s, kind, h, start, stop):
+            win = w3_window(s % NM, kind, h)
+            nc.tensor.matmul_mx(
+                out=out,
+                lhsT=w3c[:, win].bitcast(FP8X4),
+                lhsT_scale=w3s[:, win],
+                rhs=c2[s][:, HALF * h:HALF * (h + 1)].bitcast(FP8X4),
+                rhs_scale=sc2[s][:, HALF * h:HALF * (h + 1)],
+                start=start, stop=stop,
             )
 
-        def st_js(s):
-            sqs[s] = work.tile([P, 4, O], F32, name="sqs", tag="sqs", bufs=2)
-            ab = work.tile([P, 4, O], F32, name="ab", tag="ab", bufs=2)
-            exs[s] = work.tile([P, 4, O], F32, name="exs", tag="exs", bufs=2)
-            nc.scalar.activation(out=ab[:], in_=ys[s][:, :, O:O2], func=ACT.Abs)
-            nc.scalar.activation(out=sqs[s][:], in_=ys[s][:, :, 0:O], func=ACT.Square)
-            nc.scalar.activation(out=exs[s][:], in_=ab[:], func=ACT.Exp, scale=-1.0)
+        def st_h(s):
+            xy[s] = s2.tile([P, 2, HALF], F32, name="xy", tag="xy")
+            for kind in range(2):
+                for h in range(2):
+                    stage2_pass(xy[s][:, kind, :], s, kind, h, h == 0, h == 1)
+
+        def st_hsum(c):
+            psums[c] = aux.tile([P, HALF], F32, name="psum_all", tag="xw")
+            for m in range(NM):
+                for h in range(2):
+                    stage2_pass(psums[c][:], c * NM + m, 0, h, m == 0 and h == 0, m == NM - 1 and h == 1)
+
+        def bias_prep():
+            bt = aux.tile([P, P], BF16, name="bt", tag="xw")
+            nc.tensor.transpose(bt[:], b3in[:], identb[:])
+            nc.vector.tensor_copy(out=b3t[:], in_=bt[:, 0:2 * NM])
+
+        def bias_sums():
+            nc.vector.tensor_scalar(
+                out=nbr[:], in0=b3t[:, NM:2 * NM], scalar1=-1.0, scalar2=None, op0=ALU.mult)
+            nc.vector.tensor_reduce(
+                out=bs[:], in_=b3t[:].rearrange("p (x m) -> p x m", x=2),
+                axis=mybir.AxisListType.X, op=ALU.add)
+
+        def bias_consts():
+            nc.vector.tensor_scalar(
+                out=bbar[:], in0=bs[:, 0:1], scalar1=0.2, scalar2=None, op0=ALU.mult)
+            nc.vector.tensor_scalar(
+                out=vlo[:], in0=bs[:, 1:2], scalar1=-0.2, scalar2=-1e-6, op0=ALU.mult, op1=ALU.add)
+            nc.vector.tensor_scalar(
+                out=vadd[:], in0=bs[:, 1:2], scalar1=0.2, scalar2=2e-6, op0=ALU.mult, op1=ALU.add)
+
+        def st_abs(s):
+            m = s % NM
+            abs_[s] = work.tile([P, HALF], F32, name="ab", tag="ab", bufs=3)
+            nc.scalar.activation(
+                out=abs_[s][:], in_=xy[s][:, 1, :], func=ACT.Abs, bias=b3t[:, NM + m:NM + m + 1], scale=1.0)
+
+        def st_sq(s):
+            m = s % NM
+            sqs[s] = work.tile([P, HALF], F32, name="sqs", tag="sqs", bufs=3)
+            nc.scalar.activation(
+                out=sqs[s][:], in_=xy[s][:, 0, :], func=ACT.Square, bias=b3t[:, m:m + 1], scale=1.0)
+
+        def st_jx(s):
+            exs[s] = work.tile([P, HALF], F32, name="exs", tag="exs", bufs=3)
+            nc.scalar.activation(out=exs[s][:], in_=abs_[s][:], func=ACT.Exp, scale=-1.0)
+
+        def st_jr(s):
+            c, m = s // NM, s % NM
+            if m == 0:
+                accs[c] = work.tile([P, HALF], F32, name="accs", tag="accs", bufs=2)
+                nc.vector.tensor_scalar(
+                    out=accs[c][:], in0=xy[s][:, 1, :], scalar1=nbr[:, m:m + 1], scalar2=None, op0=ALU.max)
+                return
+            nc.vector.scalar_tensor_tensor(
+                out=accs[c][:], in0=xy[s][:, 1, :], scalar=nbr[:, m:m + 1], in1=accs[c][:],
+                op0=ALU.max, op1=ALU.add)
+
+        def st_prod(s):
+            c, m = s // NM, s % NM
+            if m == 0:
+                nc.vector.tensor_scalar(
+                    out=accp[:, c], in0=exs[s][:], scalar1=1.0, scalar2=None, op0=ALU.add)
+            else:
+                nc.vector.scalar_tensor_tensor(
+                    out=accp[:, c], in0=exs[s][:], scalar=1.0, in1=accp[:, c], op0=ALU.add, op1=ALU.mult)
+
+        def st_addsq(s):
+            c = s // NM
+            nc.vector.tensor_tensor(out=accs[c][:], in0=sqs[s][:], in1=accs[c][:], op=ALU.add)
 
         def st_mean(c):
-            means[c] = work.tile([P, 4, O], F32, name="mean_sb", tag="mean_sb", bufs=2)
-            msqs[c] = work.tile([P, 4, O], F32, name="msq", tag="msq", bufs=2)
-            nc.vector.scalar_tensor_tensor(
-                out=means[c][:], in0=psums[c][:, :, 0:O], scalar=0.2,
-                in1=bbar[:].to_broadcast([P, 4, O]), op0=ALU.mult, op1=ALU.add)
+            means[c] = work.tile([P, HALF], F32, name="mean_t", tag="mean_t", bufs=2)
+            msqs[c] = work.tile([P, HALF], F32, name="msq", tag="msq", bufs=2)
+            nc.vector.tensor_scalar(
+                out=means[c][:], in0=psums[c][:], scalar1=0.2, scalar2=bbar[:, 0:1],
+                op0=ALU.mult, op1=ALU.add)
+
+        def turn(pool, tag, src):
+            tt = pool.tile([P, 2, P], F32, name="tt_%s" % tag, tag=tag)
+            for jj in range(2):
+                nc.tensor.transpose(tt[:, jj, :], src[:, P * jj:P * (jj + 1)], ident[:])
+            return tt
+
+        def turned_out(on_scalar, dst, tt):
+            o = dst.rearrange("p (h jj) o -> p jj h o", jj=2)
+            i = tt[:].rearrange("p jj (h o) -> p jj h o", h=2)
+            if on_scalar:
+                nc.scalar.copy(out=o, in_=i)
+            else:
+                nc.vector.tensor_copy(out=o, in_=i)
+
+        def st_mean_t(c):
+            mts[c] = turn(aux, "xw", means[c])
+
+        def st_mean_out(c):
+            mo = work.tile([P, 4, O], F32, name="mean_sb", tag="mean_sb", bufs=2)
+            turned_out(False, mo[:], mts[c])
             nc.sync.dma_start(
-                out=out_0[c * CH:(c + 1) * CH, :].rearrange("(p j) o -> p j o", j=4),
-                in_=means[c][:])
+                out=out_0[c * CH:(c + 1) * CH, :].rearrange("(p j) o -> p j o", j=4), in_=mo[:])
 
         def st_msq(c):
             nc.vector.tensor_tensor(out=msqs[c][:], in0=means[c][:], in1=means[c][:], op=ALU.mult)
@@ -276,24 +355,8 @@ def tile_gaussianmixturemlp_pa_kernel(tc, h1, W2, b2, W3, b3, out_0, out_1):
                 out=upre[:, c], in0=accs[c][:], scalar=0.2, in1=msqs[c][:],
                 op0=ALU.mult, op1=ALU.subtract)
 
-        def st_jv(s):
-            c, m = s // NM, s % NM
-            v = ys[s][:, :, O:O2]
-            if m == 0:
-                accs[c] = work.tile([P, 4, O], F32, name="accs", tag="accs", bufs=2)
-                nc.vector.tensor_scalar(
-                    out=accp[:, c], in0=exs[s][:], scalar1=1.0, scalar2=None, op0=ALU.add)
-                nc.vector.scalar_tensor_tensor(
-                    out=accs[c][:], in0=v, scalar=0.0, in1=sqs[s][:], op0=ALU.max, op1=ALU.add)
-                return
-            nc.vector.scalar_tensor_tensor(
-                out=accs[c][:], in0=v, scalar=0.0, in1=accs[c][:], op0=ALU.max, op1=ALU.add)
-            nc.vector.scalar_tensor_tensor(
-                out=accp[:, c], in0=exs[s][:], scalar=1.0, in1=accp[:, c], op0=ALU.add, op1=ALU.mult)
-            nc.vector.tensor_tensor(out=accs[c][:], in0=sqs[s][:], in1=accs[c][:], op=ALU.add)
-
         def flat(t, c0, c1_):
-            return t[:, c0:c1_].rearrange("p c j o -> p (c j o)")
+            return t[:, c0:c1_].rearrange("p c n -> p (c n)")
 
         def fin_ln(c0, c1_):
             nc.scalar.activation(out=flat(lnp, c0, c1_), in_=flat(accp, c0, c1_), func=ACT.Ln)
@@ -305,14 +368,19 @@ def tile_gaussianmixturemlp_pa_kernel(tc, h1, W2, b2, W3, b3, out_0, out_1):
 
         def fin_v(c0, c1_):
             nc.vector.tensor_scalar(
-                out=flat(var_sb, c0, c1_), in0=flat(wv, c0, c1_), scalar1=-1e-6, scalar2=2e-6,
+                out=flat(var_t, c0, c1_), in0=flat(wv, c0, c1_), scalar1=vlo[:, 0:1], scalar2=vadd[:, 0:1],
                 op0=ALU.max, op1=ALU.add)
+
+        def fin_store(c0, c1_):
             nc.sync.dma_start(
                 out=out_1.rearrange("(c p j) o -> p c (j o)", c=NCH, j=4)[:, c0:c1_, :],
                 in_=var_sb[:, c0:c1_].rearrange("p c j o -> p c (j o)"))
 
         def w2_t(m, half):
-            xt_w[(m, half)] = transposes(aux, "xw", words_of(raw_w2[m]), 512 * half, 2)
+            if m == 0:
+                xt_w[(m, half)] = transposes(s1, "bank", words_of(raw_w2[m]), 512 * half, 2)
+            else:
+                xt_w[(m, half)] = transposes(aux, "xw", words_of(raw_w2[m]), 512 * half, 2)
             if half == 1:
                 freed()
 
@@ -329,62 +397,57 @@ def tile_gaussianmixturemlp_pa_kernel(tc, h1, W2, b2, W3, b3, out_0, out_1):
 
         def w3_prep(q):
             count = min(2, NM - 2 * q)
-            ncols = P * count
             w = w3raw[:].rearrange("p m k -> p (m k)").bitcast(F32)
             xt = transposes(aux, "xw", w, 512 * q, count)
-            copy_out(False, w3g, 256 * q, xt, ncols)
-            nc.vector.quantize_mx(
-                out=w3c[:, 256 * q:256 * q + ncols].bitcast(FP8X4),
-                scales=w3s[:, 256 * q:256 * q + ncols],
-                in_=w3g[:].rearrange("p n t -> p (n t)")[:, 1024 * q:1024 * q + 4 * ncols],
-            )
+            copy_out(False, w3g, 256 * q, xt, P * count)
+
+        def w3_q(q):
+            for m in range(2 * q, min(2 * q + 2, NM)):
+                for kind in range(2):
+                    c0 = O * (4 * m + 2 * kind + 1)
+                    g0 = 4 * (O2 * m + O * kind)
+                    nc.vector.quantize_mx(
+                        out=w3c[:, c0:c0 + O].bitcast(FP8X4), scales=w3s[:, c0:c0 + O],
+                        in_=w3g[:].rearrange("p n t -> p (n t)")[:, g0:g0 + 4 * O],
+                    )
 
         def ok(s):
             return 0 <= s < NS
 
+        def last_of_chunk(s):
+            return ok(s) and s % NM == NM - 1
+
         pump()
-        plain_dummy(6)
+        plain_dummy(4)
         w2_t(0, 0)
-        w2_copy(0, 0)
-        plain_dummy(2)
         w2_t(0, 1)
+        w2_copy(0, 0)
         w2_copy(0, 1)
-        w2_q(0)
-        plain_dummy(2)
         st_a(0, 0)
         st_a(0, 1)
-        plain_dummy(2)
-        for k in range(-1, NS + 3):
+        w2_q(0)
+        for k in range(-1, NS + 1):
             wm = k + 1
             has_w = 1 <= wm < NM
-            chunk_mean = ok(k - 2) and (k - 2) % NM == NM - 1
             if ok(k + 1):
                 st_b(k + 1)
-            if k == 0:
-                nc.scalar.dma_start(
-                    out=b3b[:].rearrange("p m o -> p (m o)"),
-                    in_=b3.rearrange("m o -> (m o)").partition_broadcast(P),
-                )
-            if ok(k - 2) and k < NS:
-                st_i(k - 2)
-            if ok(k - 4) and (k - 4) % NM == NM - 1:
+            if last_of_chunk(k - 4):
                 st_u((k - 4) // NM)
-            if k == 3:
-                bias_mean()
-            if chunk_mean and k < NS:
-                st_mean((k - 2) // NM)
             if ok(k - 1):
                 st_f(k - 1)
-            if ok(k - 2) and k >= NS:
-                st_i(k - 2)
-            if chunk_mean and k >= NS:
-                st_mean((k - 2) // NM)
             if ok(k + 1):
                 st_c(k + 1)
-            if chunk_mean and k < NS:
-                st_msq((k - 2) // NM)
+            if ok(k - 2):
+                st_abs(k - 2)
+                st_sq(k - 2)
+                st_jr(k - 2)
+            if last_of_chunk(k - 2):
+                st_mean((k - 2) // NM)
+            if last_of_chunk(k - 3):
+                st_mean_out((k - 3) // NM)
             if ok(k):
                 st_d(k, [0, 1])
+                st_e(k, [0, 1])
             if has_w:
                 w2_t(wm, 0)
                 w2_copy(wm, 0)
@@ -399,30 +462,65 @@ def tile_gaussianmixturemlp_pa_kernel(tc, h1, W2, b2, W3, b3, out_0, out_1):
                 st_g(k - 1)
             if has_w:
                 w2_q(wm)
+            if last_of_chunk(k - 2):
+                st_msq((k - 2) // NM)
             if ok(k + 2):
                 st_a(k + 2, 1)
             if ok(k):
                 st_d(k, [3])
             if 0 <= k < 3:
                 w3_prep(k)
+            if k == 0:
+                bias_prep()
             if ok(k - 1):
                 st_h(k - 1)
-                if (k - 1) % NM == NM - 1:
+                if last_of_chunk(k - 1):
                     st_hsum((k - 1) // NM)
-            if k < 0:
-                plain_dummy(2)
+            if last_of_chunk(k - 2):
+                st_mean_t((k - 2) // NM)
             if ok(k - 3):
-                st_js(k - 3)
+                st_jx(k - 3)
             if ok(k):
-                st_e(k)
+                st_e(k, [2, 3])
+            if k == 0:
+                bias_sums()
+            if 0 <= k < 3:
+                w3_q(k)
+            if k == 0:
+                bias_consts()
             if ok(k - 3):
-                st_jv(k - 3)
-            if chunk_mean and k >= NS:
-                st_msq((k - 2) // NM)
-        st_u(NCH - 1)
-        fin_ln(0, NCH - 1)
-        fin_ln(NCH - 1, NCH)
-        fin_w(0, NCH - 1)
-        fin_w(NCH - 1, NCH)
-        fin_v(0, NCH - 1)
-        fin_v(NCH - 1, NCH)
+                st_prod(k - 3)
+                st_addsq(k - 3)
+        last = NS - 1
+        cl = NCH - 1
+        st_abs(last)
+        st_jx(last - 1)
+        st_jx(last)
+        st_jr(last)
+        st_prod(last - 1)
+        st_prod(last)
+        fin_ln(0, cl)
+        st_sq(last)
+        fin_ln(cl, NCH)
+        st_addsq(last - 1)
+        st_mean(cl)
+        st_mean_t(cl)
+        fin_w(0, cl)
+        st_msq(cl)
+        fin_v(0, cl)
+        vts = {}
+        vts[0] = turn(tp, "xt", var_t[:, 0])
+        vts[1] = turn(tp, "xt", var_t[:, 1])
+        st_addsq(last)
+        st_mean_out(cl)
+        st_u(cl)
+        turned_out(True, var_sb[:, 0], vts[0])
+        turned_out(True, var_sb[:, 1], vts[1])
+        vts[2] = turn(tp, "xt", var_t[:, 2])
+        fin_w(cl, NCH)
+        turned_out(True, var_sb[:, 2], vts[2])
+        fin_store(0, cl)
+        fin_v(cl, NCH)
+        vts[3] = turn(s2, "xy", var_t[:, 3])
+        turned_out(False, var_sb[:, 3], vts[3])
+        fin_store(cl, NCH)

@@ -215,7 +215,9 @@ def tile_gaussianmixturemlp_pa_kernel(tc, h1, W2, b2, W3, b3, out_0, out_1):
 
         def st_f(s):
             g2[s] = work.tile([P, CH, 4], BF16, name="g2", tag="g2", bufs=2, align_bytes=64)
-            nc.vector.tensor_copy(out=g2[s][:], in_=h2raw[s][:].rearrange("p t n -> p n t"))
+            nc.vector.tensor_copy(
+                out=g2[s][:].rearrange("p (c i) t -> p c t i", i=4),
+                in_=h2raw[s][:].rearrange("p t (c i) -> p c t i", i=4))
 
         def st_g(s):
             c2[s] = work.tile([P, CH], U32, name="c2", tag="c2", bufs=7, align_bytes=64)

@@ -33,10 +33,9 @@ def tile_gaussianmixturemlp_pa_kernel(tc, h1, W2, b2, W3, b3, out_0, out_1):
         const = ctx.enter_context(tc.tile_pool(name="const", bufs=1))
         rawp = ctx.enter_context(tc.tile_pool(name="rawp", bufs=RAW_BUFS))
         work = ctx.enter_context(tc.tile_pool(name="work", bufs=2))
-        tp = ctx.enter_context(tc.psum_pool(name="tp", bufs=2))
-        s1 = ctx.enter_context(tc.psum_pool(name="s1", bufs=4))
+        tp = ctx.enter_context(tc.psum_pool(name="tp", bufs=4))
+        s1 = ctx.enter_context(tc.psum_pool(name="s1", bufs=3))
         s2 = ctx.enter_context(tc.psum_pool(name="s2", bufs=1))
-        aux = ctx.enter_context(tc.psum_pool(name="aux", bufs=1))
         ctx.enter_context(tc.manual_schedule())
 
         ident = const.tile([P, P], F32, name="ident", tag="ident")
@@ -254,13 +253,13 @@ def tile_gaussianmixturemlp_pa_kernel(tc, h1, W2, b2, W3, b3, out_0, out_1):
                     stage2_pass(xy[s][:, kind, :], s, kind, h, h == 0, h == 1)
 
         def st_hsum(c):
-            psums[c] = aux.tile([P, HALF], F32, name="psum_all", tag="xw")
+            psums[c] = tp.tile([P, HALF], F32, name="psum_all", tag="xt")
             for m in range(NM):
                 for h in range(2):
                     stage2_pass(psums[c][:], c * NM + m, 0, h, m == 0 and h == 0, m == NM - 1 and h == 1)
 
         def bias_prep():
-            bt = aux.tile([P, P], BF16, name="bt", tag="xw")
+            bt = tp.tile([P, P], BF16, name="bt", tag="xt")
             nc.tensor.transpose(bt[:], b3in[:], identb[:])
             nc.vector.tensor_copy(out=b3t[:], in_=bt[:, 0:2 * NM])
 
@@ -341,7 +340,7 @@ def tile_gaussianmixturemlp_pa_kernel(tc, h1, W2, b2, W3, b3, out_0, out_1):
                 nc.vector.tensor_copy(out=o, in_=i)
 
         def st_mean_t(c):
-            mts[c] = turn(aux, "xw", means[c])
+            mts[c] = turn(tp, "xt", means[c])
 
         def st_mean_out(c):
             mo = work.tile([P, 4, O], F32, name="mean_sb", tag="mean_sb", bufs=2)
@@ -382,7 +381,7 @@ def tile_gaussianmixturemlp_pa_kernel(tc, h1, W2, b2, W3, b3, out_0, out_1):
             if m == 0:
                 xt_w[(m, half)] = transposes(s1, "bank", words_of(raw_w2[m]), 512 * half, 2)
             else:
-                xt_w[(m, half)] = transposes(aux, "xw", words_of(raw_w2[m]), 512 * half, 2)
+                xt_w[(m, half)] = transposes(tp, "xt", words_of(raw_w2[m]), 512 * half, 2)
             if half == 1:
                 freed()
 
@@ -400,7 +399,7 @@ def tile_gaussianmixturemlp_pa_kernel(tc, h1, W2, b2, W3, b3, out_0, out_1):
         def w3_prep(q):
             count = min(2, NM - 2 * q)
             w = w3raw[:].rearrange("p m k -> p (m k)").bitcast(F32)
-            xt = transposes(aux, "xw", w, 512 * q, count)
+            xt = transposes(tp, "xt", w, 512 * q, count)
             copy_out(False, w3g, 256 * q, xt, P * count)
 
         def w3_q(q):

@@ -102,15 +102,18 @@ def tile_gaussianmixturemlp_pa_kernel(tc, h1, W2, b2, W3, b3, out_0, out_1):
                     state["slots"] = state["slots"] - 1
                     t = rawp.tile([P, 4, H], BF16, name="raw_%s%d" % (kind, i), tag="raw")
                     if kind == "w2":
-                        nc.sync.dma_start(out=t[:], in_=W2[i].rearrange("(p t) k -> p t k", t=4))
+                        src = W2[i].rearrange("(p t) k -> p t k", t=4)
                         raw_w2[i] = t
                     else:
                         c, m = i // NM, i % NM
-                        nc.sync.dma_start(
-                            out=t[:],
-                            in_=h1[m, c * CH:(c + 1) * CH, :].rearrange("(p j) k -> p j k", j=4),
-                        )
+                        src = h1[m, c * CH:(c + 1) * CH, :].rearrange("(p j) k -> p j k", j=4)
                         raw_h1[i] = t
+                    if i == 0:
+                        for half in range(2):
+                            nc.sync.dma_start(
+                                out=t[:, 2 * half:2 * half + 2, :], in_=src[:, 2 * half:2 * half + 2, :])
+                    else:
+                        nc.sync.dma_start(out=t[:], in_=src)
                 state["next"] = state["next"] + 1
 
         def freed():
@@ -342,9 +345,9 @@ def tile_gaussianmixturemlp_pa_kernel(tc, h1, W2, b2, W3, b3, out_0, out_1):
         def st_mean_t(c):
             mts[c] = turn(tp, "xt", means[c])
 
-        def st_mean_out(c):
+        def st_mean_out(c, on_scalar=False):
             mo = work.tile([P, 4, O], F32, name="mean_sb", tag="mean_sb", bufs=2)
-            turned_out(False, mo[:], mts[c])
+            turned_out(on_scalar, mo[:], mts[c])
             nc.sync.dma_start(
                 out=out_0[c * CH:(c + 1) * CH, :].rearrange("(p j) o -> p j o", j=4), in_=mo[:])
 
@@ -447,26 +450,22 @@ def tile_gaussianmixturemlp_pa_kernel(tc, h1, W2, b2, W3, b3, out_0, out_1):
             if last_of_chunk(k - 3):
                 st_mean_out((k - 3) // NM)
             if ok(k):
-                st_d(k, [0, 1])
+                st_d(k, [0, 1, 2])
                 st_e(k, [0, 1])
             if has_w:
                 w2_t(wm, 0)
                 w2_copy(wm, 0)
-            if ok(k + 2):
-                st_a(k + 2, 0)
-            if ok(k):
-                st_d(k, [2])
-            if has_w:
                 w2_t(wm, 1)
                 w2_copy(wm, 1)
+            if ok(k + 2):
+                st_a(k + 2, 0)
+                st_a(k + 2, 1)
             if ok(k - 1):
                 st_g(k - 1)
             if has_w:
                 w2_q(wm)
             if last_of_chunk(k - 2):
                 st_msq((k - 2) // NM)
-            if ok(k + 2):
-                st_a(k + 2, 1)
             if ok(k):
                 st_d(k, [3])
             if 0 <= k < 3:
@@ -481,6 +480,8 @@ def tile_gaussianmixturemlp_pa_kernel(tc, h1, W2, b2, W3, b3, out_0, out_1):
                 st_mean_t((k - 2) // NM)
             if ok(k - 3):
                 st_jx(k - 3)
+            if k == NS:
+                st_jx(k - 2)
             if ok(k):
                 st_e(k, [2, 3])
             if k == 0:
@@ -492,36 +493,36 @@ def tile_gaussianmixturemlp_pa_kernel(tc, h1, W2, b2, W3, b3, out_0, out_1):
             if ok(k - 3):
                 st_prod(k - 3)
                 st_addsq(k - 3)
+            if k == NS:
+                st_prod(k - 2)
+                st_addsq(k - 2)
         last = NS - 1
         cl = NCH - 1
         st_abs(last)
-        st_jx(last - 1)
         st_jx(last)
-        st_jr(last)
-        st_prod(last - 1)
-        st_prod(last)
-        fin_ln(0, cl)
         st_sq(last)
-        fin_ln(cl, NCH)
-        st_addsq(last - 1)
+        st_jr(last)
+        st_prod(last)
+        fin_ln(0, 2)
+        fin_ln(2, NCH)
+        st_addsq(last)
         st_mean(cl)
         st_mean_t(cl)
-        fin_w(0, cl)
         st_msq(cl)
-        fin_v(0, cl)
+        fin_w(0, 2)
+        st_u(cl)
+        fin_v(0, 2)
+        fin_w(2, NCH)
         vts = {}
         vts[0] = turn(tp, "xt", var_t[:, 0])
         vts[1] = turn(tp, "xt", var_t[:, 1])
-        st_addsq(last)
-        st_mean_out(cl)
-        st_u(cl)
+        st_mean_out(cl, True)
+        fin_v(2, NCH)
         turned_out(True, var_sb[:, 0], vts[0])
         turned_out(True, var_sb[:, 1], vts[1])
+        fin_store(0, 2)
         vts[2] = turn(tp, "xt", var_t[:, 2])
-        fin_w(cl, NCH)
+        vts[3] = turn(tp, "xt", var_t[:, 3])
         turned_out(True, var_sb[:, 2], vts[2])
-        fin_store(0, cl)
-        fin_v(cl, NCH)
-        vts[3] = turn(s2, "xy", var_t[:, 3])
         turned_out(False, var_sb[:, 3], vts[3])
-        fin_store(cl, NCH)
+        fin_store(2, NCH)

@@ -62,6 +62,10 @@ def tile_gaussianmixturemlp_pa_kernel(tc, h1, W2, b2, W3, b3, out_0, out_1):
         wv = const.tile([P, NCH, HALF], F32, name="wv", tag="wv")
         var_t = const.tile([P, NCH, HALF], F32, name="var_t", tag="var_t")
         var_sb = const.tile([P, NCH, 4, O], F32, name="var_sb", tag="var_sb")
+        mean_all = const.tile([P, NCH, HALF], F32, name="mean_all", tag="mean_all")
+        accs_all = const.tile([P, NCH, HALF], F32, name="accs_all", tag="accs_all")
+        msq_all = const.tile([P, NCH, HALF], F32, name="msq_all", tag="msq_all")
+        mean_sb = const.tile([P, NCH, 4, O], F32, name="mean_sb", tag="mean_sb")
 
         zl = const.tile([P, P], BF16, name="zl", tag="zl")
         zr = const.tile([P, CH], BF16, name="zr", tag="zr")
@@ -204,7 +208,7 @@ def tile_gaussianmixturemlp_pa_kernel(tc, h1, W2, b2, W3, b3, out_0, out_1):
             if ts[0] == 0:
                 h2raw[s] = work.tile([P, 4, CH], BF16, name="h2raw", tag="h2raw", bufs=3)
             for t in ts:
-                if t == 3 and s >= VFROM:
+                if s >= VFROM and (t == 3 or (t == 2 and s % NM in (1, 3))):
                     nc.vector.tensor_scalar(
                         out=h2raw[s][:, t, :], in0=bank[s][t][:], scalar1=b2c[:, m, t:t + 1], scalar2=0.0,
                         op0=ALU.add, op1=ALU.max,
@@ -300,12 +304,12 @@ def tile_gaussianmixturemlp_pa_kernel(tc, h1, W2, b2, W3, b3, out_0, out_1):
         def st_jr(s):
             c, m = s // NM, s % NM
             if m == 0:
-                accs[c] = work.tile([P, HALF], F32, name="accs", tag="accs", bufs=2)
+                accs[c] = accs_all[:, c]
                 nc.vector.tensor_scalar(
-                    out=accs[c][:], in0=xy[s][:, 1, :], scalar1=nbr[:, m:m + 1], scalar2=None, op0=ALU.max)
+                    out=accs[c], in0=xy[s][:, 1, :], scalar1=nbr[:, m:m + 1], scalar2=None, op0=ALU.max)
                 return
             nc.vector.scalar_tensor_tensor(
-                out=accs[c][:], in0=xy[s][:, 1, :], scalar=nbr[:, m:m + 1], in1=accs[c][:],
+                out=accs[c], in0=xy[s][:, 1, :], scalar=nbr[:, m:m + 1], in1=accs[c],
                 op0=ALU.max, op1=ALU.add)
 
         def st_prod(s):
@@ -319,13 +323,12 @@ def tile_gaussianmixturemlp_pa_kernel(tc, h1, W2, b2, W3, b3, out_0, out_1):
 
         def st_addsq(s):
             c = s // NM
-            nc.vector.tensor_tensor(out=accs[c][:], in0=sqs[s][:], in1=accs[c][:], op=ALU.add)
+            nc.vector.tensor_tensor(out=accs[c], in0=sqs[s][:], in1=accs[c], op=ALU.add)
 
         def st_mean(c):
-            means[c] = work.tile([P, HALF], F32, name="mean_t", tag="mean_t", bufs=2)
-            msqs[c] = work.tile([P, HALF], F32, name="msq", tag="msq", bufs=2)
+            means[c] = mean_all[:, c]
             nc.vector.tensor_scalar(
-                out=means[c][:], in0=psums[c][:], scalar1=0.2, scalar2=bbar[:, 0:1],
+                out=means[c], in0=psums[c][:], scalar1=0.2, scalar2=bbar[:, 0:1],
                 op0=ALU.mult, op1=ALU.add)
 
         def turn(pool, tag, src):
@@ -345,18 +348,20 @@ def tile_gaussianmixturemlp_pa_kernel(tc, h1, W2, b2, W3, b3, out_0, out_1):
         def st_mean_t(c):
             mts[c] = turn(tp, "xt", means[c])
 
-        def st_mean_out(c, on_scalar=False):
-            mo = work.tile([P, 4, O], F32, name="mean_sb", tag="mean_sb", bufs=2)
-            turned_out(on_scalar, mo[:], mts[c])
+        def st_mean_out(c, on_scalar=True):
+            turned_out(on_scalar, mean_sb[:, c], mts[c])
+
+        def mean_store(c0, c1_):
             nc.sync.dma_start(
-                out=out_0[c * CH:(c + 1) * CH, :].rearrange("(p j) o -> p j o", j=4), in_=mo[:])
+                out=out_0.rearrange("(c p j) o -> p c (j o)", c=NCH, j=4)[:, c0:c1_, :],
+                in_=mean_sb[:, c0:c1_].rearrange("p c j o -> p c (j o)"))
 
-        def st_msq(c):
-            nc.vector.tensor_tensor(out=msqs[c][:], in0=means[c][:], in1=means[c][:], op=ALU.mult)
+        def st_msq(c0, c1_):
+            nc.scalar.activation(out=flat(msq_all, c0, c1_), in_=flat(mean_all, c0, c1_), func=ACT.Square)
 
-        def st_u(c):
+        def st_u(c0, c1_):
             nc.vector.scalar_tensor_tensor(
-                out=upre[:, c], in0=accs[c][:], scalar=0.2, in1=msqs[c][:],
+                out=flat(upre, c0, c1_), in0=flat(accs_all, c0, c1_), scalar=0.2, in1=flat(msq_all, c0, c1_),
                 op0=ALU.mult, op1=ALU.subtract)
 
         def flat(t, c0, c1_):
@@ -435,8 +440,6 @@ def tile_gaussianmixturemlp_pa_kernel(tc, h1, W2, b2, W3, b3, out_0, out_1):
             has_w = 1 <= wm < NM
             if ok(k + 1):
                 st_b(k + 1)
-            if last_of_chunk(k - 4):
-                st_u((k - 4) // NM)
             if ok(k - 1):
                 st_f(k - 1)
             if ok(k + 1):
@@ -447,8 +450,6 @@ def tile_gaussianmixturemlp_pa_kernel(tc, h1, W2, b2, W3, b3, out_0, out_1):
                 st_jr(k - 2)
             if last_of_chunk(k - 2):
                 st_mean((k - 2) // NM)
-            if last_of_chunk(k - 3):
-                st_mean_out((k - 3) // NM)
             if ok(k):
                 st_d(k, [0, 1, 2])
                 st_e(k, [0, 1])
@@ -464,24 +465,27 @@ def tile_gaussianmixturemlp_pa_kernel(tc, h1, W2, b2, W3, b3, out_0, out_1):
                 st_g(k - 1)
             if has_w:
                 w2_q(wm)
-            if last_of_chunk(k - 2):
-                st_msq((k - 2) // NM)
             if ok(k):
                 st_d(k, [3])
             if 0 <= k < 3:
                 w3_prep(k)
             if k == 0:
                 bias_prep()
+            if k == NS:
+                for c in range(NCH - 1):
+                    st_mean_t(c)
             if ok(k - 1):
                 st_h(k - 1)
                 if last_of_chunk(k - 1):
                     st_hsum((k - 1) // NM)
-            if last_of_chunk(k - 2):
-                st_mean_t((k - 2) // NM)
             if ok(k - 3):
                 st_jx(k - 3)
             if k == NS:
                 st_jx(k - 2)
+                st_msq(0, NCH - 1)
+                for c in range(NCH - 1):
+                    st_mean_out(c)
+                mean_store(0, NCH - 1)
             if ok(k):
                 st_e(k, [2, 3])
             if k == 0:
@@ -496,6 +500,7 @@ def tile_gaussianmixturemlp_pa_kernel(tc, h1, W2, b2, W3, b3, out_0, out_1):
             if k == NS:
                 st_prod(k - 2)
                 st_addsq(k - 2)
+                st_u(0, NCH - 1)
         last = NS - 1
         cl = NCH - 1
         st_abs(last)
@@ -508,15 +513,16 @@ def tile_gaussianmixturemlp_pa_kernel(tc, h1, W2, b2, W3, b3, out_0, out_1):
         st_addsq(last)
         st_mean(cl)
         st_mean_t(cl)
-        st_msq(cl)
         fin_w(0, 2)
-        st_u(cl)
+        st_msq(cl, NCH)
         fin_v(0, 2)
+        st_u(cl, NCH)
         fin_w(2, NCH)
         vts = {}
         vts[0] = turn(tp, "xt", var_t[:, 0])
         vts[1] = turn(tp, "xt", var_t[:, 1])
-        st_mean_out(cl, True)
+        st_mean_out(cl)
+        mean_store(cl, NCH)
         fin_v(2, NCH)
         turned_out(True, var_sb[:, 0], vts[0])
         turned_out(True, var_sb[:, 1], vts[1])

@@ -1,3 +1,4 @@
+import math
 from contextlib import ExitStack
 
 import concourse.mybir as mybir
@@ -25,6 +26,8 @@ VFROM = 4
 W3COLS = O * (4 * NM + 1)
 RAW_BUFS = 8
 BANK_DT = BF16
+CLAMP = 16.0
+DELTA = 1.0 / (1.0 + math.e ** CLAMP)
 
 
 def tile_gaussianmixturemlp_pa_kernel(tc, h1, W2, b2, W3, b3, out_0, out_1):
@@ -46,6 +49,7 @@ def tile_gaussianmixturemlp_pa_kernel(tc, h1, W2, b2, W3, b3, out_0, out_1):
         b3in = const.tile([P, P], BF16, name="b3in", tag="b3in")
         b3t = const.tile([P, 2 * NM], F32, name="b3t", tag="b3t")
         nbr = const.tile([P, NM], F32, name="nbr", tag="nbr")
+        cbr = const.tile([P, NM], F32, name="cbr", tag="cbr")
         bs = const.tile([P, 2], F32, name="bs", tag="bs")
         bbar = const.tile([P, 1], F32, name="bbar", tag="bbar")
         vlo = const.tile([P, 1], F32, name="vlo", tag="vlo")
@@ -75,7 +79,7 @@ def tile_gaussianmixturemlp_pa_kernel(tc, h1, W2, b2, W3, b3, out_0, out_1):
         nc.vector.memset(b3in[:], 0.0)
         nc.vector.memset(w3c[:].bitcast(I32), 0)
         nc.vector.memset(w3s[:].bitcast(I32), 0)
-        nc.scalar.activation(out=warm2[:], in_=warm[:], func=ACT.Exp)
+        nc.scalar.activation(out=warm2[:], in_=warm[:], func=ACT.Sigmoid)
         make_identity(nc, ident[:])
         make_identity(nc, identb[:])
         nc.scalar.dma_start(out=b2c[:], in_=b2.rearrange("m (p t) -> p m t", t=4))
@@ -156,7 +160,6 @@ def tile_gaussianmixturemlp_pa_kernel(tc, h1, W2, b2, W3, b3, out_0, out_1):
         c2 = {}
         sc2 = {}
         xy = {}
-        abs_ = {}
         sqs = {}
         exs = {}
         accs = {}
@@ -208,7 +211,7 @@ def tile_gaussianmixturemlp_pa_kernel(tc, h1, W2, b2, W3, b3, out_0, out_1):
             if ts[0] == 0:
                 h2raw[s] = work.tile([P, 4, CH], BF16, name="h2raw", tag="h2raw", bufs=3)
             for t in ts:
-                if s >= VFROM and (t == 3 or (t == 2 and s % NM in (1, 3))):
+                if s >= VFROM and t == 3:
                     nc.vector.tensor_scalar(
                         out=h2raw[s][:, t, :], in0=bank[s][t][:], scalar1=b2c[:, m, t:t + 1], scalar2=0.0,
                         op0=ALU.add, op1=ALU.max,
@@ -273,6 +276,8 @@ def tile_gaussianmixturemlp_pa_kernel(tc, h1, W2, b2, W3, b3, out_0, out_1):
         def bias_sums():
             nc.vector.tensor_scalar(
                 out=nbr[:], in0=b3t[:, NM:2 * NM], scalar1=-1.0, scalar2=None, op0=ALU.mult)
+            nc.vector.tensor_scalar(
+                out=cbr[:], in0=b3t[:, NM:2 * NM], scalar1=-1.0, scalar2=CLAMP, op0=ALU.mult, op1=ALU.add)
             nc.vector.tensor_reduce(
                 out=bs[:], in_=b3t[:].rearrange("p (x m) -> p x m", x=2),
                 axis=mybir.AxisListType.X, op=ALU.add)
@@ -281,15 +286,9 @@ def tile_gaussianmixturemlp_pa_kernel(tc, h1, W2, b2, W3, b3, out_0, out_1):
             nc.vector.tensor_scalar(
                 out=bbar[:], in0=bs[:, 0:1], scalar1=0.2, scalar2=None, op0=ALU.mult)
             nc.vector.tensor_scalar(
-                out=vlo[:], in0=bs[:, 1:2], scalar1=-0.2, scalar2=-1e-6, op0=ALU.mult, op1=ALU.add)
+                out=vlo[:], in0=bs[:, 1:2], scalar1=-0.2, scalar2=CLAMP - 1e-6, op0=ALU.mult, op1=ALU.add)
             nc.vector.tensor_scalar(
-                out=vadd[:], in0=bs[:, 1:2], scalar1=0.2, scalar2=2e-6, op0=ALU.mult, op1=ALU.add)
-
-        def st_abs(s):
-            m = s % NM
-            abs_[s] = work.tile([P, HALF], F32, name="ab", tag="ab", bufs=3)
-            nc.scalar.activation(
-                out=abs_[s][:], in_=xy[s][:, 1, :], func=ACT.Abs, bias=b3t[:, NM + m:NM + m + 1], scale=1.0)
+                out=vadd[:], in0=bs[:, 1:2], scalar1=0.2, scalar2=2e-6 - CLAMP, op0=ALU.mult, op1=ALU.add)
 
         def st_sq(s):
             m = s % NM
@@ -297,29 +296,31 @@ def tile_gaussianmixturemlp_pa_kernel(tc, h1, W2, b2, W3, b3, out_0, out_1):
             nc.scalar.activation(
                 out=sqs[s][:], in_=xy[s][:, 0, :], func=ACT.Square, bias=b3t[:, m:m + 1], scale=1.0)
 
-        def st_jx(s):
+        def st_sig(s):
+            m = s % NM
             exs[s] = work.tile([P, HALF], F32, name="exs", tag="exs", bufs=3)
-            nc.scalar.activation(out=exs[s][:], in_=abs_[s][:], func=ACT.Exp, scale=-1.0)
+            nc.scalar.activation(
+                out=exs[s][:], in_=xy[s][:, 1, :], func=ACT.Sigmoid, bias=nbr[:, m:m + 1], scale=-1.0)
 
         def st_jr(s):
             c, m = s // NM, s % NM
             if m == 0:
                 accs[c] = accs_all[:, c]
                 nc.vector.tensor_scalar(
-                    out=accs[c], in0=xy[s][:, 1, :], scalar1=nbr[:, m:m + 1], scalar2=None, op0=ALU.max)
+                    out=accs[c], in0=xy[s][:, 1, :], scalar1=cbr[:, m:m + 1], scalar2=None, op0=ALU.max)
                 return
             nc.vector.scalar_tensor_tensor(
-                out=accs[c], in0=xy[s][:, 1, :], scalar=nbr[:, m:m + 1], in1=accs[c],
+                out=accs[c], in0=xy[s][:, 1, :], scalar=cbr[:, m:m + 1], in1=accs[c],
                 op0=ALU.max, op1=ALU.add)
 
         def st_prod(s):
             c, m = s // NM, s % NM
             if m == 0:
                 nc.vector.tensor_scalar(
-                    out=accp[:, c], in0=exs[s][:], scalar1=1.0, scalar2=None, op0=ALU.add)
+                    out=accp[:, c], in0=exs[s][:], scalar1=DELTA, scalar2=None, op0=ALU.max)
             else:
                 nc.vector.scalar_tensor_tensor(
-                    out=accp[:, c], in0=exs[s][:], scalar=1.0, in1=accp[:, c], op0=ALU.add, op1=ALU.mult)
+                    out=accp[:, c], in0=exs[s][:], scalar=DELTA, in1=accp[:, c], op0=ALU.max, op1=ALU.mult)
 
         def st_addsq(s):
             c = s // NM
@@ -372,7 +373,7 @@ def tile_gaussianmixturemlp_pa_kernel(tc, h1, W2, b2, W3, b3, out_0, out_1):
 
         def fin_w(c0, c1_):
             nc.vector.scalar_tensor_tensor(
-                out=flat(wv, c0, c1_), in0=flat(lnp, c0, c1_), scalar=0.2, in1=flat(upre, c0, c1_),
+                out=flat(wv, c0, c1_), in0=flat(lnp, c0, c1_), scalar=-0.2, in1=flat(upre, c0, c1_),
                 op0=ALU.mult, op1=ALU.add)
 
         def fin_v(c0, c1_):
@@ -445,7 +446,7 @@ def tile_gaussianmixturemlp_pa_kernel(tc, h1, W2, b2, W3, b3, out_0, out_1):
             if ok(k + 1):
                 st_c(k + 1)
             if ok(k - 2):
-                st_abs(k - 2)
+                st_sig(k - 2)
                 st_sq(k - 2)
                 st_jr(k - 2)
             if last_of_chunk(k - 2):
@@ -478,10 +479,7 @@ def tile_gaussianmixturemlp_pa_kernel(tc, h1, W2, b2, W3, b3, out_0, out_1):
                 st_h(k - 1)
                 if last_of_chunk(k - 1):
                     st_hsum((k - 1) // NM)
-            if ok(k - 3):
-                st_jx(k - 3)
             if k == NS:
-                st_jx(k - 2)
                 st_msq(0, NCH - 1)
                 for c in range(NCH - 1):
                     st_mean_out(c)
@@ -503,8 +501,7 @@ def tile_gaussianmixturemlp_pa_kernel(tc, h1, W2, b2, W3, b3, out_0, out_1):
                 st_u(0, NCH - 1)
         last = NS - 1
         cl = NCH - 1
-        st_abs(last)
-        st_jx(last)
+        st_sig(last)
         st_sq(last)
         st_jr(last)
         st_prod(last)

@@ -39,7 +39,7 @@ def tile_gaussianmixturemlp_pa_kernel(tc, h1, W2, b2, W3, b3, out_0, out_1):
         tp = ctx.enter_context(tc.psum_pool(name="tp", bufs=4))
         s1 = ctx.enter_context(tc.psum_pool(name="s1", bufs=3))
         s2 = ctx.enter_context(tc.psum_pool(name="s2", bufs=1))
-        ctx.enter_context(tc.manual_schedule())
+        ctx.enter_context(tc.manual_schedule(engines={mybir.EngineType.PE, mybir.EngineType.Activation}))
 
         ident = const.tile([P, P], F32, name="ident", tag="ident")
         warm = const.tile([P, 1], F32, name="warm", tag="warm")

import math
from contextlib import ExitStack

import concourse.mybir as mybir
from concourse.masks import make_identity

NM, B, H, O = 5, 2048, 512, 64
O2 = 2 * O
FLOPS = 2 * NM * B * H * (H + O2)

F32 = mybir.dt.float32
BF16 = mybir.dt.bfloat16
U32 = mybir.dt.uint32
U8 = mybir.dt.uint8
I32 = mybir.dt.int32
FP8X4 = mybir.dt.float8_e4m3fn_x4
ACT = mybir.ActivationFunctionType
ALU = mybir.AluOpType

P = 128
CH = 512
NCH = B // CH
NS = NCH * NM
HALF = CH // 2
VFROM = 4
W3COLS = O * (4 * NM + 1)
RAW_BUFS = 8
BANK_DT = BF16
CLAMP = 16.0
DELTA = 1.0 / (1.0 + math.e ** CLAMP)


def tile_gaussianmixturemlp_pa_kernel(tc, h1, W2, b2, W3, b3, out_0, out_1):
    nc = tc.nc
    with ExitStack() as ctx:
        const = ctx.enter_context(tc.tile_pool(name="const", bufs=1))
        rawp = ctx.enter_context(tc.tile_pool(name="rawp", bufs=RAW_BUFS))
        work = ctx.enter_context(tc.tile_pool(name="work", bufs=2))
        tp = ctx.enter_context(tc.psum_pool(name="tp", bufs=4))
        s1 = ctx.enter_context(tc.psum_pool(name="s1", bufs=3))
        s2 = ctx.enter_context(tc.psum_pool(name="s2", bufs=1))
        ctx.enter_context(tc.manual_schedule(engines={mybir.EngineType.PE, mybir.EngineType.Activation}))

        ident = const.tile([P, P], F32, name="ident", tag="ident")
        warm = const.tile([P, 1], F32, name="warm", tag="warm")
        warm2 = const.tile([P, 1], F32, name="warm2", tag="warm2")
        b2c = const.tile([P, NM, 4], BF16, name="b2c", tag="b2c")
        identb = const.tile([P, P], BF16, name="identb", tag="identb")
        b3in = const.tile([P, P], BF16, name="b3in", tag="b3in")
        b3t = const.tile([P, 2 * NM], F32, name="b3t", tag="b3t")
        nbr = const.tile([P, NM], F32, name="nbr", tag="nbr")
        cbr = const.tile([P, NM], F32, name="cbr", tag="cbr")
        bs = const.tile([P, 2], F32, name="bs", tag="bs")
        bbar = const.tile([P, 1], F32, name="bbar", tag="bbar")
        vlo = const.tile([P, 1], F32, name="vlo", tag="vlo")
        vadd = const.tile([P, 1], F32, name="vadd", tag="vadd")
        w3raw = const.tile([P, NM, H], BF16, name="w3raw", tag="w3raw")
        w3g = const.tile([P, NM * O2, 4], BF16, name="w3g", tag="w3g", align_bytes=64)
        w2c = const.tile([P, NM, H], U32, name="w2c", tag="w2c", align_bytes=64)
        w2s = const.tile([P, NM, H], U8, name="w2s", tag="w2s", align_bytes=64)
        w3c = const.tile([P, W3COLS], U32, name="w3c", tag="w3c", align_bytes=64)
        w3s = const.tile([P, W3COLS], U8, name="w3s", tag="w3s", align_bytes=64)
        accp = const.tile([P, NCH, HALF], F32, name="accp", tag="accp")
        upre = const.tile([P, NCH, HALF], F32, name="upre", tag="upre")
        lnp = const.tile([P, NCH, HALF], F32, name="lnp", tag="lnp")
        wv = const.tile([P, NCH, HALF], F32, name="wv", tag="wv")
        var_t = const.tile([P, NCH, HALF], F32, name="var_t", tag="var_t")
        var_sb = const.tile([P, NCH, 4, O], F32, name="var_sb", tag="var_sb")
        mean_all = const.tile([P, NCH, HALF], F32, name="mean_all", tag="mean_all")
        accs_all = const.tile([P, NCH, HALF], F32, name="accs_all", tag="accs_all")
        msq_all = const.tile([P, NCH, HALF], F32, name="msq_all", tag="msq_all")
        mean_sb = const.tile([P, NCH, 4, O], F32, name="mean_sb", tag="mean_sb")

        zl = const.tile([P, P], BF16, name="zl", tag="zl")
        zr = const.tile([P, CH], BF16, name="zr", tag="zr")
        nc.vector.memset(zl[:], 0.0)
        nc.vector.memset(zr[:], 0.0)
        nc.vector.memset(warm[:], 0.0)
        nc.vector.memset(b3in[:], 0.0)
        nc.vector.memset(w3c[:].bitcast(I32), 0)
        nc.vector.memset(w3s[:].bitcast(I32), 0)
        nc.scalar.activation(out=warm2[:], in_=warm[:], func=ACT.Sigmoid)
        make_identity(nc, ident[:])
        make_identity(nc, identb[:])
        nc.scalar.dma_start(out=b2c[:], in_=b2.rearrange("m (p t) -> p m t", t=4))
        for kind in range(2):
            for h in range(2):
                nc.scalar.dma_start(
                    out=b3in[NM * kind:NM * (kind + 1), O * h:O * (h + 1)],
                    in_=b3[:, O * kind:O * (kind + 1)])

        raw_w2 = {}
        raw_h1 = {}
        loads = [("w2", 0), ("h1", 0), ("h1", 1), ("w2", 1), ("h1", 2), ("w3", 0)]
        for i in range(2, NM):
            loads.append(("w2", i))
            loads.append(("h1", i + 1))
        for i in range(NM + 1, NS):
            loads.append(("h1", i))
        state = {"next": 0, "slots": RAW_BUFS}

        def pump():
            while state["next"] < len(loads):
                kind, i = loads[state["next"]]
                if kind == "w3":
                    nc.sync.dma_start(out=w3raw[:], in_=W3.rearrange("m o k -> o m k"))
                else:
                    if state["slots"] == 0:
                        return
                    state["slots"] = state["slots"] - 1
                    t = rawp.tile([P, 4, H], BF16, name="raw_%s%d" % (kind, i), tag="raw")
                    if kind == "w2":
                        src = W2[i].rearrange("(p t) k -> p t k", t=4)
                        raw_w2[i] = t
                    else:
                        c, m = i // NM, i % NM
                        src = h1[m, c * CH:(c + 1) * CH, :].rearrange("(p j) k -> p j k", j=4)
                        raw_h1[i] = t
                    if i == 0:
                        for half in range(2):
                            nc.sync.dma_start(
                                out=t[:, 2 * half:2 * half + 2, :], in_=src[:, 2 * half:2 * half + 2, :])
                    else:
                        nc.sync.dma_start(out=t[:], in_=src)
                state["next"] = state["next"] + 1

        def freed():
            state["slots"] = state["slots"] + 1
            pump()

        def transposes(pool, tag, words, w_first, count):
            xt = pool.tile([P, 2, 256], F32, name="xt_%s" % tag, tag=tag)
            for jj in range(count):
                w0 = w_first + 256 * jj
                for u in range(2):
                    nc.tensor.transpose(
                        xt[:, u, P * jj:P * (jj + 1)], words[:, w0 + u:w0 + 256:2], ident[:]
                    )
            return xt

        def copy_out(on_scalar, grouped, n0, xt, ncols):
            gw = grouped[:].rearrange("p n t -> p (n t)").bitcast(F32)
            dst = gw[:, 2 * n0:2 * (n0 + ncols)].rearrange("p (r u) -> p r u", u=2)
            src = xt[:, :, 0:ncols].rearrange("p u r -> p r u")
            if on_scalar:
                nc.scalar.copy(out=dst, in_=src)
            else:
                nc.vector.tensor_copy(out=dst, in_=src)

        def words_of(t):
            return t[:].rearrange("p j k -> p (j k)").bitcast(F32)

        xt_h1 = {}
        g1 = {}
        c1 = {}
        sc1 = {}
        bank = {}
        h2raw = {}
        g2 = {}
        c2 = {}
        sc2 = {}
        xy = {}
        sqs = {}
        exs = {}
        accs = {}
        psums = {}
        means = {}
        mts = {}
        msqs = {}
        wgs = {}
        xt_w = {}

        def st_a(s, half):
            if half == 0:
                xt_h1[s] = []
            xt_h1[s].append(transposes(tp, "xt", words_of(raw_h1[s]), 512 * half, 2))
            if half == 1:
                freed()

        def st_b(s):
            g1[s] = work.tile([P, CH, 4], BF16, name="g1", tag="g1", bufs=2, align_bytes=64)
            for half in range(2):
                copy_out(True, g1[s], 256 * half, xt_h1[s][half], 256)

        def st_c(s):
            c1[s] = work.tile([P, CH], U32, name="c1", tag="c1", bufs=3, align_bytes=64)
            sc1[s] = work.tile([P, CH], U8, name="sc1", tag="sc1", bufs=3, align_bytes=64)
            nc.vector.quantize_mx(
                out=c1[s][:].bitcast(FP8X4), scales=sc1[s][:],
                in_=g1[s][:].rearrange("p n t -> p (n t)"),
            )

        def st_d(s, ts):
            m = s % NM
            if ts[0] == 0:
                bank[s] = []
            for t in ts:
                ps = s1.tile([P, CH], BANK_DT, name="bank", tag="bank")
                nc.tensor.matmul_mx(
                    out=ps[:],
                    lhsT=w2c[:, m, P * t:P * (t + 1)].bitcast(FP8X4),
                    lhsT_scale=w2s[:, m, P * t:P * (t + 1)],
                    rhs=c1[s][:].bitcast(FP8X4),
                    rhs_scale=sc1[s][:],
                    start=True, stop=True,
                )
                bank[s].append(ps)

        def st_e(s, ts):
            m = s % NM
            if ts[0] == 0:
                h2raw[s] = work.tile([P, 4, CH], BF16, name="h2raw", tag="h2raw", bufs=3)
            for t in ts:
                if s >= VFROM and t == 3:
                    nc.vector.tensor_scalar(
                        out=h2raw[s][:, t, :], in0=bank[s][t][:], scalar1=b2c[:, m, t:t + 1], scalar2=0.0,
                        op0=ALU.add, op1=ALU.max,
                    )
                else:
                    nc.scalar.activation(
                        out=h2raw[s][:, t, :], in_=bank[s][t][:], func=ACT.Relu,
                        bias=b2c[:, m, t:t + 1], scale=1.0,
                    )

        def st_f(s):
            g2[s] = work.tile([P, CH, 4], BF16, name="g2", tag="g2", bufs=2, align_bytes=64)
            nc.vector.tensor_copy(
                out=g2[s][:].rearrange("p (c i) t -> p c t i", i=4),
                in_=h2raw[s][:].rearrange("p t (c i) -> p c t i", i=4))

        def st_g(s):
            c2[s] = work.tile([P, CH], U32, name="c2", tag="c2", bufs=7, align_bytes=64)
            sc2[s] = work.tile([P, CH], U8, name="sc2", tag="sc2", bufs=7, align_bytes=64)
            nc.vector.quantize_mx(
                out=c2[s][:].bitcast(FP8X4), scales=sc2[s][:],
                in_=g2[s][:].rearrange("p n t -> p (n t)"),
            )

        def plain_dummy(n):
            for i in range(n):
                junk = s1.tile([P, CH], F32, name="junk", tag="bank")
                nc.tensor.matmul(out=junk[:], lhsT=zl[:], rhs=zr[:], start=True, stop=True)

        def w3_window(m, kind, h):
            c0 = O * (4 * m + 2 * kind + 1 - h)
            return slice(c0, c0 + P)

        def stage2_pass(out, s, kind, h, start, stop):
            win = w3_window(s % NM, kind, h)
            nc.tensor.matmul_mx(
                out=out,
                lhsT=w3c[:, win].bitcast(FP8X4),
                lhsT_scale=w3s[:, win],
                rhs=c2[s][:, HALF * h:HALF * (h + 1)].bitcast(FP8X4),
                rhs_scale=sc2[s][:, HALF * h:HALF * (h + 1)],
                start=start, stop=stop,
            )

        def st_h(s):
            xy[s] = s2.tile([P, 2, HALF], F32, name="xy", tag="xy")
            for kind in range(2):
                for h in range(2):
                    stage2_pass(xy[s][:, kind, :], s, kind, h, h == 0, h == 1)

        def st_hsum(c):
            psums[c] = tp.tile([P, HALF], F32, name="psum_all", tag="xt")
            for m in range(NM):
                for h in range(2):
                    stage2_pass(psums[c][:], c * NM + m, 0, h, m == 0 and h == 0, m == NM - 1 and h == 1)

        def bias_prep():
            bt = tp.tile([P, P], BF16, name="bt", tag="xt")
            nc.tensor.transpose(bt[:], b3in[:], identb[:])
            nc.vector.tensor_copy(out=b3t[:], in_=bt[:, 0:2 * NM])

        def bias_sums():
            nc.vector.tensor_scalar(
                out=nbr[:], in0=b3t[:, NM:2 * NM], scalar1=-1.0, scalar2=None, op0=ALU.mult)
            nc.vector.tensor_scalar(
                out=cbr[:], in0=b3t[:, NM:2 * NM], scalar1=-1.0, scalar2=CLAMP, op0=ALU.mult, op1=ALU.add)
            nc.vector.tensor_reduce(
                out=bs[:], in_=b3t[:].rearrange("p (x m) -> p x m", x=2),
                axis=mybir.AxisListType.X, op=ALU.add)

        def bias_consts():
            nc.vector.tensor_scalar(
                out=bbar[:], in0=bs[:, 0:1], scalar1=0.2, scalar2=None, op0=ALU.mult)
            nc.vector.tensor_scalar(
                out=vlo[:], in0=bs[:, 1:2], scalar1=-0.2, scalar2=CLAMP - 1e-6, op0=ALU.mult, op1=ALU.add)
            nc.vector.tensor_scalar(
                out=vadd[:], in0=bs[:, 1:2], scalar1=0.2, scalar2=2e-6 - CLAMP, op0=ALU.mult, op1=ALU.add)

        def st_sq(s):
            m = s % NM
            sqs[s] = work.tile([P, HALF], F32, name="sqs", tag="sqs", bufs=3)
            nc.scalar.activation(
                out=sqs[s][:], in_=xy[s][:, 0, :], func=ACT.Square, bias=b3t[:, m:m + 1], scale=1.0)

        def st_sig(s):
            m = s % NM
            exs[s] = work.tile([P, HALF], F32, name="exs", tag="exs", bufs=3)
            nc.scalar.activation(
                out=exs[s][:], in_=xy[s][:, 1, :], func=ACT.Sigmoid, bias=nbr[:, m:m + 1], scale=-1.0)

        def st_jr(s):
            c, m = s // NM, s % NM
            if m == 0:
                accs[c] = accs_all[:, c]
                nc.vector.tensor_scalar(
                    out=accs[c], in0=xy[s][:, 1, :], scalar1=cbr[:, m:m + 1], scalar2=None, op0=ALU.max)
                return
            nc.vector.scalar_tensor_tensor(
                out=accs[c], in0=xy[s][:, 1, :], scalar=cbr[:, m:m + 1], in1=accs[c],
                op0=ALU.max, op1=ALU.add)

        def st_prod(s):
            c, m = s // NM, s % NM
            if m == 0:
                nc.vector.tensor_scalar(
                    out=accp[:, c], in0=exs[s][:], scalar1=DELTA, scalar2=None, op0=ALU.max)
            else:
                nc.vector.scalar_tensor_tensor(
                    out=accp[:, c], in0=exs[s][:], scalar=DELTA, in1=accp[:, c], op0=ALU.max, op1=ALU.mult)

        def st_addsq(s):
            c = s // NM
            nc.vector.tensor_tensor(out=accs[c], in0=sqs[s][:], in1=accs[c], op=ALU.add)

        def st_mean(c):
            means[c] = mean_all[:, c]
            nc.vector.tensor_scalar(
                out=means[c], in0=psums[c][:], scalar1=0.2, scalar2=bbar[:, 0:1],
                op0=ALU.mult, op1=ALU.add)

        def turn(pool, tag, src):
            tt = pool.tile([P, 2, P], F32, name="tt_%s" % tag, tag=tag)
            for jj in range(2):
                nc.tensor.transpose(tt[:, jj, :], src[:, P * jj:P * (jj + 1)], ident[:])
            return tt

        def turned_out(on_scalar, dst, tt):
            o = dst.rearrange("p (h jj) o -> p jj h o", jj=2)
            i = tt[:].rearrange("p jj (h o) -> p jj h o", h=2)
            if on_scalar:
                nc.scalar.copy(out=o, in_=i)
            else:
                nc.vector.tensor_copy(out=o, in_=i)

        def st_mean_t(c):
            mts[c] = turn(tp, "xt", means[c])

        def st_mean_out(c, on_scalar=True):
            turned_out(on_scalar, mean_sb[:, c], mts[c])

        def mean_store(c0, c1_):
            nc.sync.dma_start(
                out=out_0.rearrange("(c p j) o -> p c (j o)", c=NCH, j=4)[:, c0:c1_, :],
                in_=mean_sb[:, c0:c1_].rearrange("p c j o -> p c (j o)"))

        def st_msq(c0, c1_):
            nc.scalar.activation(out=flat(msq_all, c0, c1_), in_=flat(mean_all, c0, c1_), func=ACT.Square)

        def st_u(c0, c1_):
            nc.vector.scalar_tensor_tensor(
                out=flat(upre, c0, c1_), in0=flat(accs_all, c0, c1_), scalar=0.2, in1=flat(msq_all, c0, c1_),
                op0=ALU.mult, op1=ALU.subtract)

        def flat(t, c0, c1_):
            return t[:, c0:c1_].rearrange("p c n -> p (c n)")

        def fin_ln(c0, c1_):
            nc.scalar.activation(out=flat(lnp, c0, c1_), in_=flat(accp, c0, c1_), func=ACT.Ln)

        def fin_w(c0, c1_):
            nc.vector.scalar_tensor_tensor(
                out=flat(wv, c0, c1_), in0=flat(lnp, c0, c1_), scalar=-0.2, in1=flat(upre, c0, c1_),
                op0=ALU.mult, op1=ALU.add)

        def fin_v(c0, c1_):
            nc.vector.tensor_scalar(
                out=flat(var_t, c0, c1_), in0=flat(wv, c0, c1_), scalar1=vlo[:, 0:1], scalar2=vadd[:, 0:1],
                op0=ALU.max, op1=ALU.add)

        def fin_store(c0, c1_):
            nc.sync.dma_start(
                out=out_1.rearrange("(c p j) o -> p c (j o)", c=NCH, j=4)[:, c0:c1_, :],
                in_=var_sb[:, c0:c1_].rearrange("p c j o -> p c (j o)"))

        def w2_t(m, half):
            if m == 0:
                xt_w[(m, half)] = transposes(s1, "bank", words_of(raw_w2[m]), 512 * half, 2)
            else:
                xt_w[(m, half)] = transposes(tp, "xt", words_of(raw_w2[m]), 512 * half, 2)
            if half == 1:
                freed()

        def w2_copy(m, half):
            if half == 0:
                wgs[m] = work.tile([P, H, 4], BF16, name="wg", tag="wg", bufs=2, align_bytes=64)
            copy_out(half == 0, wgs[m], 256 * half, xt_w[(m, half)], 256)

        def w2_q(m):
            nc.vector.quantize_mx(
                out=w2c[:, m, :].bitcast(FP8X4), scales=w2s[:, m, :],
                in_=wgs[m][:].rearrange("p n t -> p (n t)"),
            )

        def w3_prep(q):
            count = min(2, NM - 2 * q)
            w = w3raw[:].rearrange("p m k -> p (m k)").bitcast(F32)
            xt = transposes(tp, "xt", w, 512 * q, count)
            copy_out(False, w3g, 256 * q, xt, P * count)

        def w3_q(q):
            for m in range(2 * q, min(2 * q + 2, NM)):
                for kind in range(2):
                    c0 = O * (4 * m + 2 * kind + 1)
                    g0 = 4 * (O2 * m + O * kind)
                    nc.vector.quantize_mx(
                        out=w3c[:, c0:c0 + O].bitcast(FP8X4), scales=w3s[:, c0:c0 + O],
                        in_=w3g[:].rearrange("p n t -> p (n t)")[:, g0:g0 + 4 * O],
                    )

        def ok(s):
            return 0 <= s < NS

        def last_of_chunk(s):
            return ok(s) and s % NM == NM - 1

        pump()
        plain_dummy(4)
        w2_t(0, 0)
        w2_t(0, 1)
        w2_copy(0, 0)
        w2_copy(0, 1)
        st_a(0, 0)
        st_a(0, 1)
        w2_q(0)
        for k in range(-1, NS + 1):
            wm = k + 1
            has_w = 1 <= wm < NM
            if ok(k + 1):
                st_b(k + 1)
            if ok(k - 1):
                st_f(k - 1)
            if ok(k + 1):
                st_c(k + 1)
            if ok(k - 2):
                st_sig(k - 2)
                st_sq(k - 2)
                st_jr(k - 2)
            if last_of_chunk(k - 2):
                st_mean((k - 2) // NM)
            if ok(k):
                st_d(k, [0, 1, 2])
                st_e(k, [0, 1])
            if has_w:
                w2_t(wm, 0)
                w2_copy(wm, 0)
                w2_t(wm, 1)
                w2_copy(wm, 1)
            if ok(k + 2):
                st_a(k + 2, 0)
                st_a(k + 2, 1)
            if ok(k - 1):
                st_g(k - 1)
            if has_w:
                w2_q(wm)
            if ok(k):
                st_d(k, [3])
            if 0 <= k < 3:
                w3_prep(k)
            if k == 0:
                bias_prep()
            if k == NS:
                for c in range(NCH - 1):
                    st_mean_t(c)
            if ok(k - 1):
                st_h(k - 1)
                if last_of_chunk(k - 1):
                    st_hsum((k - 1) // NM)
            if k == NS:
                st_msq(0, NCH - 1)
                for c in range(NCH - 1):
                    st_mean_out(c)
                mean_store(0, NCH - 1)
            if ok(k):
                st_e(k, [2, 3])
            if k == 0:
                bias_sums()
            if 0 <= k < 3:
                w3_q(k)
            if k == 0:
                bias_consts()
            if ok(k - 3):
                st_prod(k - 3)
                st_addsq(k - 3)
            if k == NS:
                st_prod(k - 2)
                st_addsq(k - 2)
                st_u(0, NCH - 1)
        last = NS - 1
        cl = NCH - 1
        st_sig(last)
        st_sq(last)
        st_jr(last)
        st_prod(last)
        fin_ln(0, 2)
        fin_ln(2, NCH)
        st_addsq(last)
        st_mean(cl)
        st_mean_t(cl)
        fin_w(0, 2)
        st_msq(cl, NCH)
        fin_v(0, 2)
        st_u(cl, NCH)
        fin_w(2, NCH)
        vts = {}
        vts[0] = turn(tp, "xt", var_t[:, 0])
        vts[1] = turn(tp, "xt", var_t[:, 1])
        st_mean_out(cl)
        mean_store(cl, NCH)
        fin_v(2, NCH)
        turned_out(True, var_sb[:, 0], vts[0])
        turned_out(True, var_sb[:, 1], vts[1])
        fin_store(0, 2)
        vts[2] = turn(tp, "xt", var_t[:, 2])
        vts[3] = turn(tp, "xt", var_t[:, 3])
        turned_out(True, var_sb[:, 2], vts[2])
        turned_out(False, var_sb[:, 3], vts[3])
        fin_store(2, NCH)
